import numpy as np
import ml_dtypes


def mxq(x, axis, fmt="e4m3"):
    dtype, down = {"e4m3": (ml_dtypes.float8_e4m3fn, 7), "e5m2": (ml_dtypes.float8_e5m2, 14)}[fmt]
    v = np.moveaxis(np.asarray(x, np.float32).astype(ml_dtypes.bfloat16).astype(np.float64), axis, -1)
    blocks = v.reshape(v.shape[:-1] + (-1, 32))
    amax = np.abs(blocks).max(-1, keepdims=True)
    byte = np.maximum(np.where(amax > 0, np.frexp(amax)[1] - 1 + 127, 0) - down, 1)
    scale = np.exp2(byte - 127.0)
    codes = (blocks / scale).astype(np.float32).astype(dtype).astype(np.float64)
    return np.moveaxis((codes * scale).reshape(v.shape), -1, axis)


WIDE = False


def mx_kscale(k):
    if not WIDE:
        return np.ones(k)
    levels = np.array([10, -10, 5, -5, 0])
    a = np.random.permutation(np.resize(levels, k // 512 * 4)).reshape(k // 512, 4)
    idx = np.arange(k)
    return np.exp2(a[idx // 512, idx % 128 // 32])


BF16 = ml_dtypes.bfloat16


def bf(x):
    return np.asarray(x, np.float32).astype(BF16)


def f64(x):
    return np.asarray(x).astype(np.float64)


E2M1 = np.array([0.0, 0.5, 1.0, 1.5, 2.0, 3.0, 4.0, 6.0, -0.0, -0.5, -1.0, -1.5, -2.0, -3.0, -4.0, -6.0])


def pack_weight(w, fmt):
    k, n = w.shape
    w = f64(bf(w)).reshape(k // 32, 32, n)
    amax = np.abs(w).max(1)
    if fmt == "e4m3":
        byte = np.frexp(amax)[1] - 1 + 127 - 7
    else:
        mant, ex = np.frexp(amax / 6.0)
        byte = np.where(mant > 0.5, ex, ex - 1) + 127
    byte = np.clip(np.where(amax > 0, byte, 1), 1, 254)
    scaled = (w * np.exp2(127.0 - byte)[:, None, :]).reshape(k, n).astype(np.float32)
    by_word = np.ascontiguousarray(scaled.reshape(k // 512, 128, 4, n).transpose(0, 1, 3, 2))
    if fmt == "e4m3":
        words = by_word.astype(ml_dtypes.float8_e4m3fn).view(np.uint8)
    else:
        c = by_word.astype(ml_dtypes.float4_e2m1fn).view(np.uint8) & 0xF
        words = c[..., 0::2] | (c[..., 1::2] << 4)
    return np.ascontiguousarray(words), np.ascontiguousarray(byte.astype(np.uint8).reshape(k // 512, 16, n))


def unpack_weight(words, scales, fmt):
    g, p, n, _ = words.shape
    if fmt == "e4m3":
        vals = np.ascontiguousarray(words).view(ml_dtypes.float8_e4m3fn).astype(np.float64)
    else:
        nib = np.empty((g, p, n, 4), np.uint8)
        nib[..., 0::2] = words & 0xF
        nib[..., 1::2] = words >> 4
        vals = E2M1[nib]
    vals = vals * np.repeat(np.exp2(scales.astype(np.float64) - 127.0), 8, axis=1)[..., None]
    return vals.transpose(0, 1, 3, 2).reshape(g * 512, n)


B, S, P, F, O, DEG, R = 8, 512, 2, 512, 128, 16, 4
OC = O + O + O
FMT = "e4m3"


def rows(scale):
    return np.random.standard_normal((B, S, P, F)) * np.exp(0.4 * np.random.standard_normal((B, S, P, 1))) * scale


def setup_inputs():
    s = mx_kscale(F)
    x = bf(rows(1.0) * s)
    nb = bf(rows(1.0 / np.sqrt(DEG)) * s)
    mu = bf(rows(1.0) * s)
    wx_words, wx_scales = pack_weight((np.random.standard_normal((O, F)) / np.sqrt(F) / s).T, FMT)
    wx_b = bf(0.1 * np.random.standard_normal(O))
    wn_words, wn_scales = pack_weight((np.random.standard_normal((O, F)) / np.sqrt(F) / s).T, FMT)
    wn_b = bf(0.1 * np.random.standard_normal(O))
    wr_words, wr_scales = pack_weight((np.random.standard_normal((O, F)) / np.sqrt(F) / s).T, FMT)
    wr_b = bf(0.1 * np.random.standard_normal(O))
    return {"x": x, "nb": nb, "mu": mu,
            "Wx_w_words": wx_words, "Wx_w_scales": wx_scales, "Wx_b": wx_b,
            "Wn_w_words": wn_words, "Wn_w_scales": wn_scales, "Wn_b": wn_b,
            "Wr_w_words": wr_words, "Wr_w_scales": wr_scales, "Wr_b": wr_b,
            "bn_gamma": bf(1.0 + 0.1 * np.random.standard_normal(OC)), "bn_beta": bf(0.1 * np.random.standard_normal(OC))}


def lin(x, words, scales, b):
    return (mxq(x, 3, "e4m3") @ unpack_weight(words, scales, FMT)) + b


def reference(x, nb, mu, Wx_w_words, Wx_w_scales, Wx_b, Wn_w_words, Wn_w_scales, Wn_b, Wr_w_words, Wr_w_scales, Wr_b, bn_gamma, bn_beta):
    h = np.concatenate([lin(f64(x), Wx_w_words, Wx_w_scales, f64(Wx_b)), lin(f64(nb), Wn_w_words, Wn_w_scales, f64(Wn_b)), lin(f64(mu), Wr_w_words, Wr_w_scales, f64(Wr_b))], axis=-1)
    n = np.maximum(np.sqrt((h ** 2).sum(3, keepdims=True)), 1e-12)
    r = np.maximum(h / n, 0.0)
    m = r.mean(axis=(0, 1, 2))
    v = r.var(axis=(0, 1, 2))
    return (r - m) / np.sqrt(v + 1e-5) * f64(bn_gamma) + f64(bn_beta)

@@ -1,0 +1,219 @@
+from contextlib import ExitStack
+
+from concourse import mybir
+from concourse.masks import make_identity
+
+F32 = mybir.dt.float32
+BF16 = mybir.dt.bfloat16
+I32 = mybir.dt.int32
+U32 = mybir.dt.uint32
+U8 = mybir.dt.uint8
+FP8X4 = mybir.dt.float8_e4m3fn_x4
+ALU = mybir.AluOpType
+ACT = mybir.ActivationFunctionType
+
+P = 128
+ROWS = 8 * 512 * 2
+FEAT = 512
+CH = 128
+STREAMS = 3
+ALL_CH = STREAMS * CH
+SLOTS = 4
+CHUNK = P * SLOTS
+CHUNKS = ROWS // CHUNK
+WORDS = FEAT // 2
+BN_STATS = 6
+
+FLOPS = 2 * ROWS * FEAT * ALL_CH
+
+
+def tile_batchedgraphsagemean1_pb_t_kernel(
+    tc,
+    x, nb, mu,
+    wx_words, wx_scales, wx_b,
+    wn_words, wn_scales, wn_b,
+    wr_words, wr_scales, wr_b,
+    bn_gamma, bn_beta,
+    out,
+):
+    nc = tc.nc
+    feats = [x.flatten_outer_dims(), nb.flatten_outer_dims(), mu.flatten_outer_dims()]
+    w_words_in = [wx_words, wn_words, wr_words]
+    w_scales_in = [wx_scales, wn_scales, wr_scales]
+    biases_in = [wx_b, wn_b, wr_b]
+    out_rows = out.flatten_outer_dims()
+
+    with ExitStack() as ctx:
+        const = ctx.enter_context(tc.tile_pool(name="const", bufs=1))
+        keep = ctx.enter_context(tc.tile_pool(name="keep", bufs=1))
+
+        ident = const.tile([P, P], F32)
+        make_identity(nc, ident[:])
+
+        w_codes = const.tile([P, STREAMS, CH], U32, align_bytes=64)
+        w_planes = const.tile([P, STREAMS, CH], U8, align_bytes=64)
+        nc.vector.memset(w_planes[:].rearrange("p s n -> p (s n)").bitcast(I32), 0)
+
+        bias_bf = const.tile([P, STREAMS, CH], BF16)
+        bias_all = const.tile([P, ALL_CH], F32)
+        gb_rows_bf = const.tile([P, P], BF16)
+        gb_rows = const.tile([P, P], F32)
+        gb = const.tile([P, 2 * STREAMS], F32)
+        nc.vector.memset(gb_rows_bf[:], 0.0)
+
+        r_ch = keep.tile([P, STREAMS, ROWS], F32)
+        stats = keep.tile([P, STREAMS, CHUNKS, BN_STATS], F32)
+
+        def load_chunk(pool, c):
+            tiles = []
+            for s in range(STREAMS):
+                x_sb = pool.tile([P, SLOTS, FEAT], BF16, tag="x_sb", name="x_sb")
+                nc.sync.dma_start(
+                    out=x_sb[:],
+                    in_=feats[s][c * CHUNK:(c + 1) * CHUNK, :].rearrange("(p t) f -> p t f", t=SLOTS),
+                )
+                tiles.append(x_sb)
+            return tiles
+
+        with ExitStack() as work:
+            xin = work.enter_context(tc.tile_pool(name="xin", bufs=9))
+            quant = work.enter_context(tc.tile_pool(name="quant", bufs=6))
+            rowp = work.enter_context(tc.tile_pool(name="rowp", bufs=8))
+            small = work.enter_context(tc.tile_pool(name="small", bufs=4))
+            ps_xt = work.enter_context(tc.psum_pool(name="ps_xt", bufs=3))
+            ps_h = work.enter_context(tc.psum_pool(name="ps_h", bufs=2))
+            ps_rc = work.enter_context(tc.psum_pool(name="ps_rc", bufs=3))
+
+            first_chunk = load_chunk(xin, 0)
+
+            for s in range(STREAMS):
+                nc.sync.dma_start(
+                    out=w_codes[:, s, :].bitcast(I32),
+                    in_=w_words_in[s][0].rearrange("p n t -> p (n t)").bitcast(I32),
+                )
+            for s in range(STREAMS):
+                for quad in range(4):
+                    nc.sync.dma_start(
+                        out=w_planes[32 * quad:32 * quad + 4, s, :].bitcast(I32),
+                        in_=w_scales_in[s][0, 4 * quad:4 * quad + 4, :].bitcast(I32),
+                    )
+            for s in range(STREAMS):
+                nc.scalar.dma_start(out=bias_bf[:, s, :], in_=biases_in[s].partition_broadcast(P))
+            nc.scalar.dma_start(out=gb_rows_bf[0:STREAMS, :], in_=bn_gamma.rearrange("(s o) -> s o", s=STREAMS))
+            nc.scalar.dma_start(out=gb_rows_bf[STREAMS:2 * STREAMS, :], in_=bn_beta.rearrange("(s o) -> s o", s=STREAMS))
+            nc.vector.tensor_copy(out=bias_all[:], in_=bias_bf[:].rearrange("p s n -> p (s n)"))
+
+            nc.vector.tensor_copy(out=gb_rows[:], in_=gb_rows_bf[:])
+            gb_ps = ps_h.tile([P, P], F32, tag="h_rows", name="gb_ps")
+            nc.tensor.transpose(gb_ps[:], gb_rows[:], ident[:])
+            nc.vector.tensor_copy(out=gb[:], in_=gb_ps[:, 0:2 * STREAMS])
+
+            for c in range(CHUNKS):
+                x_tiles = first_chunk if c == 0 else load_chunk(xin, c)
+
+                codes = []
+                planes = []
+                for s in range(STREAMS):
+                    x_words = x_tiles[s][:].bitcast(F32)
+                    grouped = quant.tile([P, CHUNK * 4], BF16, align_bytes=64, tag="grouped", name="grouped")
+                    grouped_words = grouped[:].bitcast(F32)
+                    for half in range(2):
+                        xt = ps_xt.tile([P, 2, 2, P], F32, tag="xt", name="xt")
+                        for tt in range(2):
+                            for u in range(2):
+                                nc.tensor.transpose(
+                                    xt[:, tt, u, :], x_words[:, 2 * half + tt, u:WORDS:2], ident[:]
+                                )
+                        nc.scalar.copy(
+                            out=grouped_words[:, half * CHUNK:(half + 1) * CHUNK].rearrange(
+                                "q (tt r u) -> q tt r u", tt=2, u=2
+                            ),
+                            in_=xt[:].rearrange("q tt u r -> q tt r u"),
+                        )
+                    code = quant.tile([P, CHUNK], U32, align_bytes=64, tag="code", name="code")
+                    plane = quant.tile([P, CHUNK], U8, align_bytes=64, tag="plane", name="plane")
+                    nc.vector.quantize_mx(out=code[:].bitcast(FP8X4), scales=plane[:], in_=grouped[:])
+                    codes.append(code)
+                    planes.append(plane)
+
+                sumsq = small.tile([P, SLOTS], F32, tag="sumsq", name="sumsq")
+                h_biased = []
+                for t in range(SLOTS):
+                    cols = slice(t * P, (t + 1) * P)
+                    h_rows = ps_h.tile([P, ALL_CH], F32, tag="h_rows", name="h_rows")
+                    for s in range(STREAMS):
+                        nc.tensor.matmul_mx(
+                            out=h_rows[:, s * CH:(s + 1) * CH],
+                            lhsT=codes[s][:, cols].bitcast(FP8X4),
+                            lhsT_scale=planes[s][:, cols],
+                            rhs=w_codes[:, s, :].bitcast(FP8X4),
+                            rhs_scale=w_planes[:, s, :],
+                            start=True,
+                            stop=True,
+                        )
+                    hb = rowp.tile([P, ALL_CH], F32, tag="hb", name="hb")
+                    nc.vector.tensor_tensor(out=hb[:], in0=h_rows[:], in1=bias_all[:], op=ALU.add)
+                    squares = rowp.tile([P, ALL_CH], F32, tag="squares", name="squares")
+                    nc.scalar.activation(out=squares[:], in_=hb[:], func=ACT.Square, accum_out=sumsq[:, t:t + 1])
+                    h_biased.append(hb)
+
+                norm = small.tile([P, SLOTS], F32, tag="norm", name="norm")
+                inv_norm = small.tile([P, SLOTS], F32, tag="inv_norm", name="inv_norm")
+                nc.vector.tensor_scalar_max(out=norm[:], in0=sumsq[:], scalar1=1e-24)
+                nc.scalar.sqrt(out=norm[:], in_=norm[:])
+                nc.vector.reciprocal(out=inv_norm[:], in_=norm[:])
+
+                r_ps = [ps_rc.tile([P, CHUNK], F32, tag="r_ps", name="r_ps") for s in range(STREAMS)]
+                for t in range(SLOTS):
+                    r_rows = rowp.tile([P, ALL_CH], F32, tag="r_rows", name="r_rows")
+                    nc.vector.tensor_scalar(
+                        out=r_rows[:], in0=h_biased[t][:], scalar1=inv_norm[:, t:t + 1], scalar2=0.0,
+                        op0=ALU.mult, op1=ALU.max,
+                    )
+                    for s in range(STREAMS):
+                        nc.tensor.transpose(r_ps[s][:, t * P:(t + 1) * P], r_rows[:, s * CH:(s + 1) * CH], ident[:])
+                for s in range(STREAMS):
+                    r_part = r_ch[:, s, c * CHUNK:(c + 1) * CHUNK]
+                    nc.scalar.copy(out=r_part, in_=r_ps[s][:])
+                    nc.vector.bn_stats(out=stats[:, s, c, :], in_=r_part)
+
+        mean_var = const.tile([P, STREAMS, 2], F32)
+        for s in range(STREAMS):
+            nc.vector.bn_aggr(out=mean_var[:, s, :], in_=stats[:, s, :, :].rearrange("p c k -> p (c k)"))
+        std = const.tile([P, STREAMS], F32)
+        scale = const.tile([P, STREAMS], F32)
+        shift = const.tile([P, STREAMS], F32)
+        nc.vector.tensor_scalar_add(out=std[:], in0=mean_var[:, :, 1], scalar1=1e-5)
+        nc.scalar.sqrt(out=std[:], in_=std[:])
+        nc.vector.reciprocal(out=scale[:], in_=std[:])
+        nc.vector.tensor_tensor(out=scale[:], in0=scale[:], in1=gb[:, 0:STREAMS], op=ALU.mult)
+        nc.vector.tensor_tensor(out=shift[:], in0=mean_var[:, :, 0], in1=scale[:], op=ALU.mult)
+        nc.vector.tensor_tensor(out=shift[:], in0=gb[:, STREAMS:2 * STREAMS], in1=shift[:], op=ALU.subtract)
+
+        with ExitStack() as tail:
+            stage_pool = tail.enter_context(tc.tile_pool(name="stage", bufs=3))
+            ps_out = tail.enter_context(tc.psum_pool(name="ps_out", bufs=8))
+            for c in range(CHUNKS):
+                for s in range(STREAMS):
+                    r_part = r_ch[:, s, c * CHUNK:(c + 1) * CHUNK]
+                    nc.vector.tensor_scalar(
+                        out=r_part, in0=r_part, scalar1=scale[:, s:s + 1], scalar2=shift[:, s:s + 1],
+                        op0=ALU.mult, op1=ALU.add,
+                    )
+                stage = stage_pool.tile([P, SLOTS * ALL_CH], F32, tag="stage", name="stage")
+                for bank in range(STREAMS):
+                    o_ps = ps_out.tile([P, 4 * P], F32, tag="o_ps", name="o_ps")
+                    for k in range(4):
+                        t, s = divmod(4 * bank + k, STREAMS)
+                        nc.tensor.transpose(
+                            o_ps[:, k * P:(k + 1) * P], r_ch[:, s, c * CHUNK + t * P:c * CHUNK + (t + 1) * P], ident[:]
+                        )
+                    dst = stage[:, bank * 4 * P:(bank + 1) * 4 * P]
+                    if bank == 2:
+                        nc.vector.tensor_copy(out=dst, in_=o_ps[:])
+                    else:
+                        nc.scalar.copy(out=dst, in_=o_ps[:])
+                nc.sync.dma_start(
+                    out=out_rows[c * CHUNK:(c + 1) * CHUNK, :].rearrange("(p t) n -> p (t n)", t=SLOTS),
+                    in_=stage[:],
+                )

@@ -1,6 +1,6 @@
 from contextlib import ExitStack
 
-from concourse import mybir
+import concourse.mybir as mybir
 from concourse.masks import make_identity
 
 F32 = mybir.dt.float32
@@ -22,7 +22,12 @@ SLOTS = 4
 CHUNK = P * SLOTS
 CHUNKS = ROWS // CHUNK
 WORDS = FEAT // 2
+BANK = 512
+SQUARES = SLOTS * STREAMS
+PER_BANK = BANK // P
+CHUNK_BANKS = SQUARES // PER_BANK
 BN_STATS = 6
+AHEAD = 2
 
 FLOPS = 2 * ROWS * FEAT * ALL_CH
 
@@ -44,139 +49,181 @@ def tile_batchedgraphsagemean1_pb_t_kernel(
     out_rows = out.flatten_outer_dims()
 
     with ExitStack() as ctx:
+        ctx.enter_context(tc.manual_schedule())
         const = ctx.enter_context(tc.tile_pool(name="const", bufs=1))
-        keep = ctx.enter_context(tc.tile_pool(name="keep", bufs=1))
+        xin = ctx.enter_context(tc.tile_pool(name="xin", bufs=3 * STREAMS))
+        quant = ctx.enter_context(tc.tile_pool(name="quant", bufs=2 * STREAMS))
+        rowp = ctx.enter_context(tc.tile_pool(name="rowp", bufs=3))
+        small = ctx.enter_context(tc.tile_pool(name="small", bufs=4))
+        banks = ctx.enter_context(tc.psum_pool(name="banks", bufs=8))
 
         ident = const.tile([P, P], F32)
-        make_identity(nc, ident[:])
-
         w_codes = const.tile([P, STREAMS, CH], U32, align_bytes=64)
         w_planes = const.tile([P, STREAMS, CH], U8, align_bytes=64)
-        nc.vector.memset(w_planes[:].rearrange("p s n -> p (s n)").bitcast(I32), 0)
-
-        bias_bf = const.tile([P, STREAMS, CH], BF16)
-        bias_all = const.tile([P, ALL_CH], F32)
+        bias_bf = const.tile([P, ALL_CH], BF16)
+        bias_rep = const.tile([P, SLOTS, ALL_CH], F32)
         gb_rows_bf = const.tile([P, P], BF16)
         gb_rows = const.tile([P, P], F32)
         gb = const.tile([P, 2 * STREAMS], F32)
-        nc.vector.memset(gb_rows_bf[:], 0.0)
+        r_ch = const.tile([P, CHUNKS, SQUARES, P], F32)
+        stats = const.tile([P, STREAMS, CHUNKS, BN_STATS], F32)
 
-        r_ch = keep.tile([P, STREAMS, ROWS], F32)
-        stats = keep.tile([P, STREAMS, CHUNKS, BN_STATS], F32)
+        x_tiles = {}
+        grouped = {}
+        codes = {}
+        planes = {}
+        h_biased = {}
+        sumsq = {}
+        norm = {}
+        scaled = {}
 
-        def load_chunk(pool, c):
-            tiles = []
+        def load(c):
+            x_tiles[c] = []
             for s in range(STREAMS):
-                x_sb = pool.tile([P, SLOTS, FEAT], BF16, tag="x_sb", name="x_sb")
+                x_sb = xin.tile([P, SLOTS, FEAT], BF16, tag="x_sb", name="x_sb")
                 nc.sync.dma_start(
                     out=x_sb[:],
                     in_=feats[s][c * CHUNK:(c + 1) * CHUNK, :].rearrange("(p t) f -> p t f", t=SLOTS),
                 )
-                tiles.append(x_sb)
-            return tiles
+                x_tiles[c].append(x_sb)
 
-        with ExitStack() as work:
-            xin = work.enter_context(tc.tile_pool(name="xin", bufs=9))
-            quant = work.enter_context(tc.tile_pool(name="quant", bufs=6))
-            rowp = work.enter_context(tc.tile_pool(name="rowp", bufs=8))
-            small = work.enter_context(tc.tile_pool(name="small", bufs=4))
-            ps_xt = work.enter_context(tc.psum_pool(name="ps_xt", bufs=3))
-            ps_h = work.enter_context(tc.psum_pool(name="ps_h", bufs=2))
-            ps_rc = work.enter_context(tc.psum_pool(name="ps_rc", bufs=3))
-
-            first_chunk = load_chunk(xin, 0)
-
+        def features_to_partitions(c):
+            grouped[c] = []
             for s in range(STREAMS):
-                nc.sync.dma_start(
-                    out=w_codes[:, s, :].bitcast(I32),
-                    in_=w_words_in[s][0].rearrange("p n t -> p (n t)").bitcast(I32),
+                x_words = x_tiles[c][s][:].bitcast(F32)
+                g = quant.tile([P, CHUNK * 4], BF16, align_bytes=64, tag="grouped", name="grouped")
+                g_words = g[:].bitcast(F32)
+                for half in range(2):
+                    xt = banks.tile([P, 2, 2, P], F32, tag="bank", name="xt")
+                    for tt in range(2):
+                        for u in range(2):
+                            nc.tensor.transpose(xt[:, tt, u, :], x_words[:, 2 * half + tt, u:WORDS:2], ident[:])
+                    dst = g_words[:, half * BANK:(half + 1) * BANK].rearrange("q (tt r u) -> q tt r u", tt=2, u=2)
+                    src = xt[:].rearrange("q tt u r -> q tt r u")
+                    if s < 2:
+                        nc.scalar.copy(out=dst, in_=src)
+                    else:
+                        nc.vector.tensor_copy(out=dst, in_=src)
+                grouped[c].append(g)
+
+        def quantise(c):
+            codes[c] = []
+            planes[c] = []
+            for s in range(STREAMS):
+                code = quant.tile([P, CHUNK], U32, align_bytes=64, tag="code", name="code")
+                plane = quant.tile([P, CHUNK], U8, align_bytes=64, tag="plane", name="plane")
+                nc.vector.quantize_mx(out=code[:].bitcast(FP8X4), scales=plane[:], in_=grouped[c][s][:])
+                codes[c].append(code)
+                planes[c].append(plane)
+
+        def project(c):
+            hb = rowp.tile([P, SQUARES * P], F32, tag="hb", name="hb")
+            for b in range(CHUNK_BANKS):
+                h = banks.tile([P, BANK], F32, tag="bank", name="h")
+                for k in range(PER_BANK):
+                    t, s = divmod(PER_BANK * b + k, STREAMS)
+                    nc.tensor.matmul_mx(
+                        out=h[:, k * P:(k + 1) * P],
+                        lhsT=codes[c][s][:, t * P:(t + 1) * P].bitcast(FP8X4),
+                        lhsT_scale=planes[c][s][:, t * P:(t + 1) * P],
+                        rhs=w_codes[:, s, :].bitcast(FP8X4),
+                        rhs_scale=w_planes[:, s, :],
+                        start=True,
+                        stop=True,
+                    )
+                nc.vector.tensor_tensor(
+                    out=hb[:, b * BANK:(b + 1) * BANK],
+                    in0=h[:],
+                    in1=bias_rep[:].rearrange("p t n -> p (t n)")[:, b * BANK:(b + 1) * BANK],
+                    op=ALU.add,
                 )
+            h_biased[c] = hb
+
+        def sum_squares(c):
+            sumsq[c] = small.tile([P, SLOTS], F32, tag="sumsq", name="sumsq")
+            for t in range(SLOTS):
+                squares = small.tile([P, ALL_CH], F32, tag="squares", name="squares")
+                nc.scalar.activation(
+                    out=squares[:], in_=h_biased[c][:, t * ALL_CH:(t + 1) * ALL_CH], func=ACT.Square,
+                    accum_out=sumsq[c][:, t:t + 1],
+                )
+
+        def row_norm(c):
+            norm[c] = small.tile([P, SLOTS], F32, tag="norm", name="norm")
+            nc.vector.tensor_scalar_max(out=norm[c][:], in0=sumsq[c][:], scalar1=1e-24)
+            nc.scalar.sqrt(out=norm[c][:], in_=norm[c][:])
+
+        def divide_by_norm(c):
+            inv_norm = small.tile([P, SLOTS], F32, tag="inv_norm", name="inv_norm")
+            nc.vector.reciprocal(out=inv_norm[:], in_=norm[c][:])
+            z = rowp.tile([P, SQUARES * P], F32, tag="z", name="z")
+            for t in range(SLOTS):
+                nc.gpsimd.tensor_scalar(
+                    out=z[:, t * ALL_CH:(t + 1) * ALL_CH], in0=h_biased[c][:, t * ALL_CH:(t + 1) * ALL_CH],
+                    scalar1=inv_norm[:, t:t + 1], scalar2=0.0, op0=ALU.mult, op1=ALU.add,
+                )
+            scaled[c] = z
+
+        def channels_to_partitions(c):
+            for b in range(CHUNK_BANKS):
+                zt = banks.tile([P, PER_BANK, P], F32, tag="bank", name="zt")
+                for k in range(PER_BANK):
+                    j = PER_BANK * b + k
+                    nc.tensor.transpose(zt[:, k, :], scaled[c][:, j * P:(j + 1) * P], ident[:])
+                nc.scalar.activation(out=r_ch[:, c, PER_BANK * b:PER_BANK * (b + 1), :], in_=zt[:], func=ACT.Relu)
+
+        def of_stream(c, s):
+            return r_ch[:, c, :, :].rearrange("n (t s) r -> n s t r", s=STREAMS)[:, s]
+
+        def statistics(c):
             for s in range(STREAMS):
-                for quad in range(4):
-                    nc.sync.dma_start(
-                        out=w_planes[32 * quad:32 * quad + 4, s, :].bitcast(I32),
-                        in_=w_scales_in[s][0, 4 * quad:4 * quad + 4, :].bitcast(I32),
-                    )
-            for s in range(STREAMS):
-                nc.scalar.dma_start(out=bias_bf[:, s, :], in_=biases_in[s].partition_broadcast(P))
-            nc.scalar.dma_start(out=gb_rows_bf[0:STREAMS, :], in_=bn_gamma.rearrange("(s o) -> s o", s=STREAMS))
-            nc.scalar.dma_start(out=gb_rows_bf[STREAMS:2 * STREAMS, :], in_=bn_beta.rearrange("(s o) -> s o", s=STREAMS))
-            nc.vector.tensor_copy(out=bias_all[:], in_=bias_bf[:].rearrange("p s n -> p (s n)"))
+                nc.vector.bn_stats(out=stats[:, s, c, :], in_=of_stream(c, s))
 
-            nc.vector.tensor_copy(out=gb_rows[:], in_=gb_rows_bf[:])
-            gb_ps = ps_h.tile([P, P], F32, tag="h_rows", name="gb_ps")
-            nc.tensor.transpose(gb_ps[:], gb_rows[:], ident[:])
-            nc.vector.tensor_copy(out=gb[:], in_=gb_ps[:, 0:2 * STREAMS])
+        nc.vector.memset(w_planes[:].rearrange("p s n -> p (s n)").bitcast(I32), 0)
+        nc.vector.memset(gb_rows_bf[:], 0.0)
+        make_identity(nc, ident[:])
+        for c in range(AHEAD):
+            load(c)
+        for s in range(STREAMS):
+            nc.sync.dma_start(
+                out=w_codes[:, s, :].bitcast(I32),
+                in_=w_words_in[s][0].rearrange("p n t -> p (n t)").bitcast(I32),
+            )
+        for s in range(STREAMS):
+            for quad in range(4):
+                nc.sync.dma_start(
+                    out=w_planes[32 * quad:32 * quad + 4, s, :].bitcast(I32),
+                    in_=w_scales_in[s][0, 4 * quad:4 * quad + 4, :].bitcast(I32),
+                )
+        for s in range(STREAMS):
+            nc.scalar.dma_start(out=bias_bf[:, s * CH:(s + 1) * CH], in_=biases_in[s].partition_broadcast(P))
+        nc.scalar.dma_start(out=gb_rows_bf[0:STREAMS, :], in_=bn_gamma.rearrange("(s o) -> s o", s=STREAMS))
+        nc.scalar.dma_start(out=gb_rows_bf[STREAMS:2 * STREAMS, :], in_=bn_beta.rearrange("(s o) -> s o", s=STREAMS))
+        for t in range(SLOTS):
+            nc.vector.tensor_copy(out=bias_rep[:, t, :], in_=bias_bf[:])
+        nc.vector.tensor_copy(out=gb_rows[:], in_=gb_rows_bf[:])
 
-            for c in range(CHUNKS):
-                x_tiles = first_chunk if c == 0 else load_chunk(xin, c)
+        stages = [
+            row_norm,
+            statistics,
+            divide_by_norm,
+            channels_to_partitions,
+            sum_squares,
+            project,
+            quantise,
+            features_to_partitions,
+        ]
+        lags = [4, 6, 4, 5, 3, 2, 1, 0]
+        for i in range(CHUNKS + max(lags)):
+            if i + AHEAD < CHUNKS:
+                load(i + AHEAD)
+            for stage, lag in zip(stages, lags):
+                if 0 <= i - lag < CHUNKS:
+                    stage(i - lag)
 
-                codes = []
-                planes = []
-                for s in range(STREAMS):
-                    x_words = x_tiles[s][:].bitcast(F32)
-                    grouped = quant.tile([P, CHUNK * 4], BF16, align_bytes=64, tag="grouped", name="grouped")
-                    grouped_words = grouped[:].bitcast(F32)
-                    for half in range(2):
-                        xt = ps_xt.tile([P, 2, 2, P], F32, tag="xt", name="xt")
-                        for tt in range(2):
-                            for u in range(2):
-                                nc.tensor.transpose(
-                                    xt[:, tt, u, :], x_words[:, 2 * half + tt, u:WORDS:2], ident[:]
-                                )
-                        nc.scalar.copy(
-                            out=grouped_words[:, half * CHUNK:(half + 1) * CHUNK].rearrange(
-                                "q (tt r u) -> q tt r u", tt=2, u=2
-                            ),
-                            in_=xt[:].rearrange("q tt u r -> q tt r u"),
-                        )
-                    code = quant.tile([P, CHUNK], U32, align_bytes=64, tag="code", name="code")
-                    plane = quant.tile([P, CHUNK], U8, align_bytes=64, tag="plane", name="plane")
-                    nc.vector.quantize_mx(out=code[:].bitcast(FP8X4), scales=plane[:], in_=grouped[:])
-                    codes.append(code)
-                    planes.append(plane)
-
-                sumsq = small.tile([P, SLOTS], F32, tag="sumsq", name="sumsq")
-                h_biased = []
-                for t in range(SLOTS):
-                    cols = slice(t * P, (t + 1) * P)
-                    h_rows = ps_h.tile([P, ALL_CH], F32, tag="h_rows", name="h_rows")
-                    for s in range(STREAMS):
-                        nc.tensor.matmul_mx(
-                            out=h_rows[:, s * CH:(s + 1) * CH],
-                            lhsT=codes[s][:, cols].bitcast(FP8X4),
-                            lhsT_scale=planes[s][:, cols],
-                            rhs=w_codes[:, s, :].bitcast(FP8X4),
-                            rhs_scale=w_planes[:, s, :],
-                            start=True,
-                            stop=True,
-                        )
-                    hb = rowp.tile([P, ALL_CH], F32, tag="hb", name="hb")
-                    nc.vector.tensor_tensor(out=hb[:], in0=h_rows[:], in1=bias_all[:], op=ALU.add)
-                    squares = rowp.tile([P, ALL_CH], F32, tag="squares", name="squares")
-                    nc.scalar.activation(out=squares[:], in_=hb[:], func=ACT.Square, accum_out=sumsq[:, t:t + 1])
-                    h_biased.append(hb)
-
-                norm = small.tile([P, SLOTS], F32, tag="norm", name="norm")
-                inv_norm = small.tile([P, SLOTS], F32, tag="inv_norm", name="inv_norm")
-                nc.vector.tensor_scalar_max(out=norm[:], in0=sumsq[:], scalar1=1e-24)
-                nc.scalar.sqrt(out=norm[:], in_=norm[:])
-                nc.vector.reciprocal(out=inv_norm[:], in_=norm[:])
-
-                r_ps = [ps_rc.tile([P, CHUNK], F32, tag="r_ps", name="r_ps") for s in range(STREAMS)]
-                for t in range(SLOTS):
-                    r_rows = rowp.tile([P, ALL_CH], F32, tag="r_rows", name="r_rows")
-                    nc.vector.tensor_scalar(
-                        out=r_rows[:], in0=h_biased[t][:], scalar1=inv_norm[:, t:t + 1], scalar2=0.0,
-                        op0=ALU.mult, op1=ALU.max,
-                    )
-                    for s in range(STREAMS):
-                        nc.tensor.transpose(r_ps[s][:, t * P:(t + 1) * P], r_rows[:, s * CH:(s + 1) * CH], ident[:])
-                for s in range(STREAMS):
-                    r_part = r_ch[:, s, c * CHUNK:(c + 1) * CHUNK]
-                    nc.scalar.copy(out=r_part, in_=r_ps[s][:])
-                    nc.vector.bn_stats(out=stats[:, s, c, :], in_=r_part)
-
+        gb_ps = banks.tile([P, P], F32, tag="bank", name="gb_ps")
+        nc.tensor.transpose(gb_ps[:], gb_rows[:], ident[:])
+        nc.vector.tensor_copy(out=gb[:], in_=gb_ps[:, 0:2 * STREAMS])
         mean_var = const.tile([P, STREAMS, 2], F32)
         for s in range(STREAMS):
             nc.vector.bn_aggr(out=mean_var[:, s, :], in_=stats[:, s, :, :].rearrange("p c k -> p (c k)"))
@@ -190,30 +237,32 @@ def tile_batchedgraphsagemean1_pb_t_kernel(
         nc.vector.tensor_tensor(out=shift[:], in0=mean_var[:, :, 0], in1=scale[:], op=ALU.mult)
         nc.vector.tensor_tensor(out=shift[:], in0=gb[:, STREAMS:2 * STREAMS], in1=shift[:], op=ALU.subtract)
 
-        with ExitStack() as tail:
-            stage_pool = tail.enter_context(tc.tile_pool(name="stage", bufs=3))
-            ps_out = tail.enter_context(tc.psum_pool(name="ps_out", bufs=8))
-            for c in range(CHUNKS):
-                for s in range(STREAMS):
-                    r_part = r_ch[:, s, c * CHUNK:(c + 1) * CHUNK]
-                    nc.vector.tensor_scalar(
-                        out=r_part, in0=r_part, scalar1=scale[:, s:s + 1], scalar2=shift[:, s:s + 1],
-                        op0=ALU.mult, op1=ALU.add,
-                    )
-                stage = stage_pool.tile([P, SLOTS * ALL_CH], F32, tag="stage", name="stage")
-                for bank in range(STREAMS):
-                    o_ps = ps_out.tile([P, 4 * P], F32, tag="o_ps", name="o_ps")
-                    for k in range(4):
-                        t, s = divmod(4 * bank + k, STREAMS)
-                        nc.tensor.transpose(
-                            o_ps[:, k * P:(k + 1) * P], r_ch[:, s, c * CHUNK + t * P:c * CHUNK + (t + 1) * P], ident[:]
-                        )
-                    dst = stage[:, bank * 4 * P:(bank + 1) * 4 * P]
-                    if bank == 2:
-                        nc.vector.tensor_copy(out=dst, in_=o_ps[:])
-                    else:
-                        nc.scalar.copy(out=dst, in_=o_ps[:])
-                nc.sync.dma_start(
-                    out=out_rows[c * CHUNK:(c + 1) * CHUNK, :].rearrange("(p t) n -> p (t n)", t=SLOTS),
-                    in_=stage[:],
+        def scale_and_shift(c):
+            for s in range(STREAMS):
+                nc.vector.tensor_scalar(
+                    out=of_stream(c, s), in0=of_stream(c, s), scalar1=scale[:, s:s + 1], scalar2=shift[:, s:s + 1],
+                    op0=ALU.mult, op1=ALU.add,
                 )
+
+        def rows_to_partitions_and_store(c):
+            stage = rowp.tile([P, SQUARES * P], F32, tag="z", name="stage")
+            for b in range(CHUNK_BANKS):
+                o_ps = banks.tile([P, PER_BANK, P], F32, tag="bank", name="o_ps")
+                for k in range(PER_BANK):
+                    nc.tensor.transpose(o_ps[:, k, :], r_ch[:, c, PER_BANK * b + k, :], ident[:])
+                dst = stage[:, b * BANK:(b + 1) * BANK]
+                src = o_ps[:].rearrange("p k n -> p (k n)")
+                if b == CHUNK_BANKS - 1:
+                    nc.vector.tensor_copy(out=dst, in_=src)
+                else:
+                    nc.scalar.copy(out=dst, in_=src)
+            nc.sync.dma_start(
+                out=out_rows[c * CHUNK:(c + 1) * CHUNK, :].rearrange("(p t) n -> p (t n)", t=SLOTS),
+                in_=stage[:],
+            )
+
+        scale_and_shift(0)
+        for c in range(CHUNKS):
+            if c + 1 < CHUNKS:
+                scale_and_shift(c + 1)
+            rows_to_partitions_and_store(c)

@@ -207,13 +207,13 @@ def tile_batchedgraphsagemean1_pb_t_kernel(
             row_norm,
             statistics,
             divide_by_norm,
+            project,
             channels_to_partitions,
             sum_squares,
-            project,
             quantise,
             features_to_partitions,
         ]
-        lags = [4, 6, 4, 5, 3, 2, 1, 0]
+        lags = [4, 6, 4, 2, 5, 3, 1, 0]
         for i in range(CHUNKS + max(lags)):
             if i + AHEAD < CHUNKS:
                 load(i + AHEAD)

@@ -18,18 +18,25 @@ FEAT = 512
 CH = 128
 STREAMS = 3
 ALL_CH = STREAMS * CH
-SLOTS = 4
-CHUNK = P * SLOTS
-CHUNKS = ROWS // CHUNK
 WORDS = FEAT // 2
 BANK = 512
-SQUARES = SLOTS * STREAMS
 PER_BANK = BANK // P
-CHUNK_BANKS = SQUARES // PER_BANK
 BN_STATS = 6
+
+MAX_SLOTS = 4
+PIECE_SLOTS = [MAX_SLOTS] * 15 + [2, 1, 1]
+PIECES = len(PIECE_SLOTS)
+FIRST_SLOT = [sum(PIECE_SLOTS[:i]) for i in range(PIECES)]
+ALL_SLOTS = sum(PIECE_SLOTS)
+assert ALL_SLOTS * P == ROWS
 AHEAD = 2
+DEPTH = 4
 
 FLOPS = 2 * ROWS * FEAT * ALL_CH
+
+
+def bank_loads(squares):
+    return [(first, min(PER_BANK, squares - first)) for first in range(0, squares, PER_BANK)]
 
 
 def tile_batchedgraphsagemean1_pb_t_kernel(
@@ -61,12 +68,13 @@ def tile_batchedgraphsagemean1_pb_t_kernel(
         w_codes = const.tile([P, STREAMS, CH], U32, align_bytes=64)
         w_planes = const.tile([P, STREAMS, CH], U8, align_bytes=64)
         bias_bf = const.tile([P, ALL_CH], BF16)
-        bias_rep = const.tile([P, SLOTS, ALL_CH], F32)
+        bias_rep = const.tile([P, MAX_SLOTS, ALL_CH], F32)
         gb_rows_bf = const.tile([P, P], BF16)
         gb_rows = const.tile([P, P], F32)
         gb = const.tile([P, 2 * STREAMS], F32)
-        r_ch = const.tile([P, CHUNKS, SQUARES, P], F32)
-        stats = const.tile([P, STREAMS, CHUNKS, BN_STATS], F32)
+        minus_half = const.tile([P, MAX_SLOTS], F32)
+        r_ch = const.tile([P, ALL_SLOTS * STREAMS, P], F32)
+        stats = const.tile([P, STREAMS, PIECES, BN_STATS], F32)
 
         x_tiles = {}
         grouped = {}
@@ -74,116 +82,120 @@ def tile_batchedgraphsagemean1_pb_t_kernel(
         planes = {}
         h_biased = {}
         sumsq = {}
-        norm = {}
         scaled = {}
 
-        def load(c):
-            x_tiles[c] = []
-            for s in range(STREAMS):
-                x_sb = xin.tile([P, SLOTS, FEAT], BF16, tag="x_sb", name="x_sb")
-                nc.sync.dma_start(
-                    out=x_sb[:],
-                    in_=feats[s][c * CHUNK:(c + 1) * CHUNK, :].rearrange("(p t) f -> p t f", t=SLOTS),
-                )
-                x_tiles[c].append(x_sb)
+        def rows_of(i):
+            return slice(FIRST_SLOT[i] * P, (FIRST_SLOT[i] + PIECE_SLOTS[i]) * P)
 
-        def features_to_partitions(c):
-            grouped[c] = []
+        def load(i):
+            n = PIECE_SLOTS[i]
+            x_tiles[i] = []
             for s in range(STREAMS):
-                x_words = x_tiles[c][s][:].bitcast(F32)
-                g = quant.tile([P, CHUNK * 4], BF16, align_bytes=64, tag="grouped", name="grouped")
+                x_sb = xin.tile([P, MAX_SLOTS, FEAT], BF16, tag="x_sb", name="x_sb")
+                nc.sync.dma_start(out=x_sb[:, 0:n, :], in_=feats[s][rows_of(i), :].rearrange("(p t) f -> p t f", t=n))
+                x_tiles[i].append(x_sb)
+
+        def features_to_partitions(i):
+            n = PIECE_SLOTS[i]
+            grouped[i] = []
+            for s in range(STREAMS):
+                x_words = x_tiles[i][s][:].bitcast(F32)
+                g = quant.tile([P, MAX_SLOTS * P * 4], BF16, align_bytes=64, tag="grouped", name="grouped")
                 g_words = g[:].bitcast(F32)
-                for half in range(2):
-                    xt = banks.tile([P, 2, 2, P], F32, tag="bank", name="xt")
-                    for tt in range(2):
+                for first, count in bank_loads(2 * n):
+                    slots = count // 2
+                    t0 = first // 2
+                    xt = banks.tile([P, PER_BANK // 2, 2, P], F32, tag="bank", name="xt")
+                    for tt in range(slots):
                         for u in range(2):
-                            nc.tensor.transpose(xt[:, tt, u, :], x_words[:, 2 * half + tt, u:WORDS:2], ident[:])
-                    dst = g_words[:, half * BANK:(half + 1) * BANK].rearrange("q (tt r u) -> q tt r u", tt=2, u=2)
-                    src = xt[:].rearrange("q tt u r -> q tt r u")
-                    if s < 2:
-                        nc.scalar.copy(out=dst, in_=src)
-                    else:
+                            nc.tensor.transpose(xt[:, tt, u, :], x_words[:, t0 + tt, u:WORDS:2], ident[:])
+                    dst = g_words[:, first * P:(first + count) * P].rearrange("q (tt r u) -> q tt r u", tt=slots, u=2)
+                    src = xt[:, 0:slots, :, :].rearrange("q tt u r -> q tt r u")
+                    if s == STREAMS - 1 and (first > 0 or i % 2 == 0):
                         nc.vector.tensor_copy(out=dst, in_=src)
-                grouped[c].append(g)
+                    else:
+                        nc.scalar.copy(out=dst, in_=src)
+                grouped[i].append(g)
 
-        def quantise(c):
-            codes[c] = []
-            planes[c] = []
+        def quantise(i):
+            cols = PIECE_SLOTS[i] * P
+            codes[i] = []
+            planes[i] = []
             for s in range(STREAMS):
-                code = quant.tile([P, CHUNK], U32, align_bytes=64, tag="code", name="code")
-                plane = quant.tile([P, CHUNK], U8, align_bytes=64, tag="plane", name="plane")
-                nc.vector.quantize_mx(out=code[:].bitcast(FP8X4), scales=plane[:], in_=grouped[c][s][:])
-                codes[c].append(code)
-                planes[c].append(plane)
+                code = quant.tile([P, MAX_SLOTS * P], U32, align_bytes=64, tag="code", name="code")
+                plane = quant.tile([P, MAX_SLOTS * P], U8, align_bytes=64, tag="plane", name="plane")
+                nc.vector.quantize_mx(
+                    out=code[:, 0:cols].bitcast(FP8X4), scales=plane[:, 0:cols], in_=grouped[i][s][:, 0:4 * cols]
+                )
+                codes[i].append(code)
+                planes[i].append(plane)
 
-        def project(c):
-            hb = rowp.tile([P, SQUARES * P], F32, tag="hb", name="hb")
-            for b in range(CHUNK_BANKS):
+        def project(i):
+            hb = rowp.tile([P, MAX_SLOTS * ALL_CH], F32, tag="hb", name="hb")
+            for first, count in bank_loads(PIECE_SLOTS[i] * STREAMS):
                 h = banks.tile([P, BANK], F32, tag="bank", name="h")
-                for k in range(PER_BANK):
-                    t, s = divmod(PER_BANK * b + k, STREAMS)
+                for k in range(count):
+                    t, s = divmod(first + k, STREAMS)
                     nc.tensor.matmul_mx(
                         out=h[:, k * P:(k + 1) * P],
-                        lhsT=codes[c][s][:, t * P:(t + 1) * P].bitcast(FP8X4),
-                        lhsT_scale=planes[c][s][:, t * P:(t + 1) * P],
+                        lhsT=codes[i][s][:, t * P:(t + 1) * P].bitcast(FP8X4),
+                        lhsT_scale=planes[i][s][:, t * P:(t + 1) * P],
                         rhs=w_codes[:, s, :].bitcast(FP8X4),
                         rhs_scale=w_planes[:, s, :],
                         start=True,
                         stop=True,
                     )
+                cols = slice(first * P, (first + count) * P)
                 nc.vector.tensor_tensor(
-                    out=hb[:, b * BANK:(b + 1) * BANK],
-                    in0=h[:],
-                    in1=bias_rep[:].rearrange("p t n -> p (t n)")[:, b * BANK:(b + 1) * BANK],
+                    out=hb[:, cols], in0=h[:, 0:count * P], in1=bias_rep[:].rearrange("p t n -> p (t n)")[:, cols],
                     op=ALU.add,
                 )
-            h_biased[c] = hb
+            h_biased[i] = hb
 
-        def sum_squares(c):
-            sumsq[c] = small.tile([P, SLOTS], F32, tag="sumsq", name="sumsq")
-            for t in range(SLOTS):
+        def sum_squares(i):
+            sumsq[i] = small.tile([P, MAX_SLOTS], F32, tag="sumsq", name="sumsq")
+            for t in range(PIECE_SLOTS[i]):
                 squares = small.tile([P, ALL_CH], F32, tag="squares", name="squares")
                 nc.scalar.activation(
-                    out=squares[:], in_=h_biased[c][:, t * ALL_CH:(t + 1) * ALL_CH], func=ACT.Square,
-                    accum_out=sumsq[c][:, t:t + 1],
+                    out=squares[:], in_=h_biased[i][:, t * ALL_CH:(t + 1) * ALL_CH], func=ACT.Square,
+                    accum_out=sumsq[i][:, t:t + 1],
                 )
 
-        def row_norm(c):
-            norm[c] = small.tile([P, SLOTS], F32, tag="norm", name="norm")
-            nc.vector.tensor_scalar_max(out=norm[c][:], in0=sumsq[c][:], scalar1=1e-24)
-            nc.scalar.sqrt(out=norm[c][:], in_=norm[c][:])
-
-        def divide_by_norm(c):
-            inv_norm = small.tile([P, SLOTS], F32, tag="inv_norm", name="inv_norm")
-            nc.vector.reciprocal(out=inv_norm[:], in_=norm[c][:])
-            z = rowp.tile([P, SQUARES * P], F32, tag="z", name="z")
-            for t in range(SLOTS):
+        def divide_by_norm(i):
+            n = PIECE_SLOTS[i]
+            inv_norm = small.tile([P, MAX_SLOTS], F32, tag="inv_norm", name="inv_norm")
+            nc.gpsimd.tensor_scalar_max(out=inv_norm[:, 0:n], in0=sumsq[i][:, 0:n], scalar1=1e-24)
+            nc.gpsimd.tensor_tensor(out=inv_norm[:, 0:n], in0=inv_norm[:, 0:n], in1=minus_half[:, 0:n], op=ALU.pow)
+            z = rowp.tile([P, MAX_SLOTS * ALL_CH], F32, tag="z", name="z")
+            for t in range(n):
                 nc.gpsimd.tensor_scalar(
-                    out=z[:, t * ALL_CH:(t + 1) * ALL_CH], in0=h_biased[c][:, t * ALL_CH:(t + 1) * ALL_CH],
+                    out=z[:, t * ALL_CH:(t + 1) * ALL_CH], in0=h_biased[i][:, t * ALL_CH:(t + 1) * ALL_CH],
                     scalar1=inv_norm[:, t:t + 1], scalar2=0.0, op0=ALU.mult, op1=ALU.add,
                 )
-            scaled[c] = z
+            scaled[i] = z
 
-        def channels_to_partitions(c):
-            for b in range(CHUNK_BANKS):
+        def channels_to_partitions(i):
+            for first, count in bank_loads(PIECE_SLOTS[i] * STREAMS):
                 zt = banks.tile([P, PER_BANK, P], F32, tag="bank", name="zt")
-                for k in range(PER_BANK):
-                    j = PER_BANK * b + k
-                    nc.tensor.transpose(zt[:, k, :], scaled[c][:, j * P:(j + 1) * P], ident[:])
-                nc.scalar.activation(out=r_ch[:, c, PER_BANK * b:PER_BANK * (b + 1), :], in_=zt[:], func=ACT.Relu)
+                for k in range(count):
+                    nc.tensor.transpose(zt[:, k, :], scaled[i][:, (first + k) * P:(first + k + 1) * P], ident[:])
+                square = FIRST_SLOT[i] * STREAMS + first
+                nc.scalar.activation(out=r_ch[:, square:square + count, :], in_=zt[:, 0:count, :], func=ACT.Relu)
 
-        def of_stream(c, s):
-            return r_ch[:, c, :, :].rearrange("n (t s) r -> n s t r", s=STREAMS)[:, s]
+        def of_stream(i, s):
+            squares = slice(FIRST_SLOT[i] * STREAMS, (FIRST_SLOT[i] + PIECE_SLOTS[i]) * STREAMS)
+            return r_ch[:, squares, :].rearrange("n (t s) r -> n s t r", s=STREAMS)[:, s]
 
-        def statistics(c):
+        def statistics(i):
             for s in range(STREAMS):
-                nc.vector.bn_stats(out=stats[:, s, c, :], in_=of_stream(c, s))
+                nc.vector.bn_stats(out=stats[:, s, i, :], in_=of_stream(i, s))
 
         nc.vector.memset(w_planes[:].rearrange("p s n -> p (s n)").bitcast(I32), 0)
         nc.vector.memset(gb_rows_bf[:], 0.0)
         make_identity(nc, ident[:])
-        for c in range(AHEAD):
-            load(c)
+        nc.gpsimd.memset(minus_half[:], -0.5)
+        for i in range(AHEAD):
+            load(i)
         for s in range(STREAMS):
             nc.sync.dma_start(
                 out=w_codes[:, s, :].bitcast(I32),
@@ -199,31 +211,31 @@ def tile_batchedgraphsagemean1_pb_t_kernel(
             nc.scalar.dma_start(out=bias_bf[:, s * CH:(s + 1) * CH], in_=biases_in[s].partition_broadcast(P))
         nc.scalar.dma_start(out=gb_rows_bf[0:STREAMS, :], in_=bn_gamma.rearrange("(s o) -> s o", s=STREAMS))
         nc.scalar.dma_start(out=gb_rows_bf[STREAMS:2 * STREAMS, :], in_=bn_beta.rearrange("(s o) -> s o", s=STREAMS))
-        for t in range(SLOTS):
+        warm = const.tile([P, 1], F32)
+        nc.vector.memset(warm[:], 1.0)
+        nc.scalar.sqrt(out=warm[:], in_=warm[:])
+        for t in range(MAX_SLOTS):
             nc.vector.tensor_copy(out=bias_rep[:, t, :], in_=bias_bf[:])
         nc.vector.tensor_copy(out=gb_rows[:], in_=gb_rows_bf[:])
 
-        stages = [
-            row_norm,
-            statistics,
-            divide_by_norm,
-            project,
-            channels_to_partitions,
-            sum_squares,
-            quantise,
-            features_to_partitions,
-        ]
-        lags = [4, 6, 4, 2, 5, 3, 1, 0]
-        for i in range(CHUNKS + max(lags)):
-            if i + AHEAD < CHUNKS:
-                load(i + AHEAD)
-            for stage, lag in zip(stages, lags):
-                if 0 <= i - lag < CHUNKS:
-                    stage(i - lag)
+        def run(stage, i):
+            if 0 <= i < PIECES:
+                stage(i)
 
-        gb_ps = banks.tile([P, P], F32, tag="bank", name="gb_ps")
-        nc.tensor.transpose(gb_ps[:], gb_rows[:], ident[:])
-        nc.vector.tensor_copy(out=gb[:], in_=gb_ps[:, 0:2 * STREAMS])
+        for turn in range(PIECES + DEPTH):
+            run(load, turn + AHEAD)
+            run(project, turn - 2)
+            run(sum_squares, turn - 3)
+            run(divide_by_norm, turn - 3)
+            run(channels_to_partitions, turn - DEPTH)
+            run(quantise, turn - 1)
+            run(statistics, turn - DEPTH)
+            run(features_to_partitions, turn)
+            if turn == 0:
+                gb_ps = banks.tile([P, P], F32, tag="bank", name="gb_ps")
+                nc.tensor.transpose(gb_ps[:], gb_rows[:], ident[:])
+                nc.vector.tensor_copy(out=gb[:], in_=gb_ps[:, 0:2 * STREAMS])
+
         mean_var = const.tile([P, STREAMS, 2], F32)
         for s in range(STREAMS):
             nc.vector.bn_aggr(out=mean_var[:, s, :], in_=stats[:, s, :, :].rearrange("p c k -> p (c k)"))
@@ -237,32 +249,34 @@ def tile_batchedgraphsagemean1_pb_t_kernel(
         nc.vector.tensor_tensor(out=shift[:], in0=mean_var[:, :, 0], in1=scale[:], op=ALU.mult)
         nc.vector.tensor_tensor(out=shift[:], in0=gb[:, STREAMS:2 * STREAMS], in1=shift[:], op=ALU.subtract)
 
-        def scale_and_shift(c):
+        def scale_and_shift(i):
             for s in range(STREAMS):
                 nc.vector.tensor_scalar(
-                    out=of_stream(c, s), in0=of_stream(c, s), scalar1=scale[:, s:s + 1], scalar2=shift[:, s:s + 1],
+                    out=of_stream(i, s), in0=of_stream(i, s), scalar1=scale[:, s:s + 1], scalar2=shift[:, s:s + 1],
                     op0=ALU.mult, op1=ALU.add,
                 )
 
-        def rows_to_partitions_and_store(c):
-            stage = rowp.tile([P, SQUARES * P], F32, tag="z", name="stage")
-            for b in range(CHUNK_BANKS):
+        def rows_to_partitions_and_store(i):
+            n = PIECE_SLOTS[i]
+            loads = bank_loads(n * STREAMS)
+            stage = rowp.tile([P, MAX_SLOTS * ALL_CH], F32, tag="z", name="stage")
+            for first, count in loads:
                 o_ps = banks.tile([P, PER_BANK, P], F32, tag="bank", name="o_ps")
-                for k in range(PER_BANK):
-                    nc.tensor.transpose(o_ps[:, k, :], r_ch[:, c, PER_BANK * b + k, :], ident[:])
-                dst = stage[:, b * BANK:(b + 1) * BANK]
-                src = o_ps[:].rearrange("p k n -> p (k n)")
-                if b == CHUNK_BANKS - 1:
+                for k in range(count):
+                    nc.tensor.transpose(o_ps[:, k, :], r_ch[:, FIRST_SLOT[i] * STREAMS + first + k, :], ident[:])
+                dst = stage[:, first * P:(first + count) * P]
+                src = o_ps[:, 0:count, :].rearrange("p k n -> p (k n)")
+                if (first, count) == loads[-1]:
                     nc.vector.tensor_copy(out=dst, in_=src)
                 else:
                     nc.scalar.copy(out=dst, in_=src)
             nc.sync.dma_start(
-                out=out_rows[c * CHUNK:(c + 1) * CHUNK, :].rearrange("(p t) n -> p (t n)", t=SLOTS),
-                in_=stage[:],
+                out=out_rows[rows_of(i), :].rearrange("(p t) n -> p (t n)", t=n), in_=stage[:, 0:n * ALL_CH]
             )
 
-        scale_and_shift(0)
-        for c in range(CHUNKS):
-            if c + 1 < CHUNKS:
-                scale_and_shift(c + 1)
-            rows_to_partitions_and_store(c)
+        order = list(reversed(range(PIECES)))
+        scale_and_shift(order[0])
+        for k in range(PIECES):
+            if k + 1 < PIECES:
+                scale_and_shift(order[k + 1])
+            rows_to_partitions_and_store(order[k])

@@ -74,7 +74,8 @@ def tile_batchedgraphsagemean1_pb_t_kernel(
         gb = const.tile([P, 2 * STREAMS], F32)
         minus_half = const.tile([P, MAX_SLOTS], F32)
         r_ch = const.tile([P, ALL_SLOTS * STREAMS, P], F32)
-        stats = const.tile([P, STREAMS, PIECES, BN_STATS], F32)
+        stats = const.tile([P, STREAMS, PIECES - 1, BN_STATS], F32)
+        tuples = const.tile([P, STREAMS, 3, BN_STATS // 2], F32)
 
         x_tiles = {}
         grouped = {}
@@ -187,11 +188,27 @@ def tile_batchedgraphsagemean1_pb_t_kernel(
             return r_ch[:, squares, :].rearrange("n (t s) r -> n s t r", s=STREAMS)[:, s]
 
         def statistics(i):
+            if i == PIECES - 1:
+                for s in range(STREAMS):
+                    nc.vector.bn_aggr(
+                        out=tuples[:, s, 0, 1:3], in_=stats[:, s, :, :].rearrange("p c k -> p (c k)")
+                    )
+                nc.vector.tensor_scalar_mul(
+                    out=tuples[:, :, 0, 2], in0=tuples[:, :, 0, 2], scalar1=float(FIRST_SLOT[i] * P)
+                )
             for s in range(STREAMS):
-                nc.vector.bn_stats(out=stats[:, s, i, :], in_=of_stream(i, s))
+                if i == PIECES - 1:
+                    nc.vector.bn_stats(out=tuples[:, s, 1:3, :].rearrange("p a k -> p (a k)"), in_=of_stream(i, s))
+                else:
+                    nc.vector.bn_stats(out=stats[:, s, i, :], in_=of_stream(i, s))
 
         nc.vector.memset(w_planes[:].rearrange("p s n -> p (s n)").bitcast(I32), 0)
         nc.vector.memset(gb_rows_bf[:], 0.0)
+        nc.vector.memset(tuples[:], float(FIRST_SLOT[PIECES - 1] * P))
+        zero = const.tile([P, 1], F32)
+        eps = const.tile([P, 1], F32)
+        nc.vector.memset(zero[:], 0.0)
+        nc.vector.tensor_scalar_add(out=eps[:], in0=zero[:], scalar1=1e-5)
         make_identity(nc, ident[:])
         nc.gpsimd.memset(minus_half[:], -0.5)
         for i in range(AHEAD):
@@ -238,43 +255,59 @@ def tile_batchedgraphsagemean1_pb_t_kernel(
 
         mean_var = const.tile([P, STREAMS, 2], F32)
         for s in range(STREAMS):
-            nc.vector.bn_aggr(out=mean_var[:, s, :], in_=stats[:, s, :, :].rearrange("p c k -> p (c k)"))
+            nc.vector.bn_aggr(out=mean_var[:, s, :], in_=tuples[:, s, :, :].rearrange("p a k -> p (a k)"))
         std = const.tile([P, STREAMS], F32)
+        inv_std = const.tile([P, STREAMS], F32)
+        minus_mean_gamma = const.tile([P, STREAMS], F32)
         scale = const.tile([P, STREAMS], F32)
         shift = const.tile([P, STREAMS], F32)
-        nc.vector.tensor_scalar_add(out=std[:], in0=mean_var[:, :, 1], scalar1=1e-5)
-        nc.scalar.sqrt(out=std[:], in_=std[:])
-        nc.vector.reciprocal(out=scale[:], in_=std[:])
-        nc.vector.tensor_tensor(out=scale[:], in0=scale[:], in1=gb[:, 0:STREAMS], op=ALU.mult)
-        nc.vector.tensor_tensor(out=shift[:], in0=mean_var[:, :, 0], in1=scale[:], op=ALU.mult)
-        nc.vector.tensor_tensor(out=shift[:], in0=gb[:, STREAMS:2 * STREAMS], in1=shift[:], op=ALU.subtract)
+        nc.scalar.activation(out=std[:], in_=mean_var[:, :, 1], func=ACT.Sqrt, bias=eps[:, 0:1])
+        nc.vector.scalar_tensor_tensor(
+            out=minus_mean_gamma[:], in0=mean_var[:, :, 0], scalar=-1.0, in1=gb[:, 0:STREAMS], op0=ALU.mult, op1=ALU.mult
+        )
+        nc.vector.reciprocal(out=inv_std[:], in_=std[:])
+        nc.vector.tensor_tensor(out=scale[:], in0=inv_std[:], in1=gb[:, 0:STREAMS], op=ALU.mult)
+        for s in range(STREAMS):
+            nc.vector.scalar_tensor_tensor(
+                out=shift[:, s:s + 1], in0=minus_mean_gamma[:, s:s + 1], scalar=inv_std[:, s:s + 1],
+                in1=gb[:, STREAMS + s:STREAMS + s + 1], op0=ALU.mult, op1=ALU.add,
+            )
+
+        order = list(range(PIECES))
 
         def scale_and_shift(i):
             for s in range(STREAMS):
-                nc.vector.tensor_scalar(
-                    out=of_stream(i, s), in0=of_stream(i, s), scalar1=scale[:, s:s + 1], scalar2=shift[:, s:s + 1],
-                    op0=ALU.mult, op1=ALU.add,
-                )
+                if i == order[0] and s == STREAMS - 1:
+                    nc.scalar.activation(
+                        out=of_stream(i, s), in_=of_stream(i, s), func=ACT.Identity,
+                        scale=scale[:, s:s + 1], bias=shift[:, s:s + 1],
+                    )
+                else:
+                    nc.vector.tensor_scalar(
+                        out=of_stream(i, s), in0=of_stream(i, s), scalar1=scale[:, s:s + 1], scalar2=shift[:, s:s + 1],
+                        op0=ALU.mult, op1=ALU.add,
+                    )
 
         def rows_to_partitions_and_store(i):
             n = PIECE_SLOTS[i]
             loads = bank_loads(n * STREAMS)
-            stage = rowp.tile([P, MAX_SLOTS * ALL_CH], F32, tag="z", name="stage")
+            piece_out = out_rows[rows_of(i), :].rearrange("(p t) n -> p (t n)", t=n)
+            stage = rowp.tile([P, MAX_SLOTS * ALL_CH], F32, tag="z" if i % 2 == 0 else "hb", name="stage")
             for first, count in loads:
                 o_ps = banks.tile([P, PER_BANK, P], F32, tag="bank", name="o_ps")
                 for k in range(count):
                     nc.tensor.transpose(o_ps[:, k, :], r_ch[:, FIRST_SLOT[i] * STREAMS + first + k, :], ident[:])
-                dst = stage[:, first * P:(first + count) * P]
+                cols = slice(first * P, (first + count) * P)
                 src = o_ps[:, 0:count, :].rearrange("p k n -> p (k n)")
                 if (first, count) == loads[-1]:
-                    nc.vector.tensor_copy(out=dst, in_=src)
+                    nc.vector.tensor_copy(out=stage[:, cols], in_=src)
                 else:
-                    nc.scalar.copy(out=dst, in_=src)
-            nc.sync.dma_start(
-                out=out_rows[rows_of(i), :].rearrange("(p t) n -> p (t n)", t=n), in_=stage[:, 0:n * ALL_CH]
-            )
+                    nc.scalar.copy(out=stage[:, cols], in_=src)
+                if i == order[0]:
+                    nc.sync.dma_start(out=piece_out[:, cols], in_=stage[:, cols])
+            if i != order[0]:
+                nc.sync.dma_start(out=piece_out, in_=stage[:, 0:n * ALL_CH])
 
-        order = list(reversed(range(PIECES)))
         scale_and_shift(order[0])
         for k in range(PIECES):
             if k + 1 < PIECES:

@@ -106,12 +106,12 @@ def tile_batchedgraphsagemean1_pb_t_kernel(
                 for first, count in bank_loads(2 * n):
                     slots = count // 2
                     t0 = first // 2
-                    xt = banks.tile([P, PER_BANK // 2, 2, P], F32, tag="bank", name="xt")
+                    xt = banks.tile([P, PER_BANK // 2, P, 2], F32, tag="bank", name="xt")
                     for tt in range(slots):
                         for u in range(2):
-                            nc.tensor.transpose(xt[:, tt, u, :], x_words[:, t0 + tt, u:WORDS:2], ident[:])
-                    dst = g_words[:, first * P:(first + count) * P].rearrange("q (tt r u) -> q tt r u", tt=slots, u=2)
-                    src = xt[:, 0:slots, :, :].rearrange("q tt u r -> q tt r u")
+                            nc.tensor.transpose(xt[:, tt, :, u], x_words[:, t0 + tt, u:WORDS:2], ident[:])
+                    dst = g_words[:, first * P:(first + count) * P]
+                    src = xt[:, 0:slots, :, :].rearrange("q tt r u -> q (tt r u)")
                     if s == STREAMS - 1 and (first > 0 or i % 2 == 0):
                         nc.vector.tensor_copy(out=dst, in_=src)
                     else:

@@ -67,8 +67,9 @@ def tile_batchedgraphsagemean1_pb_t_kernel(
         ident = const.tile([P, P], F32)
         w_codes = const.tile([P, STREAMS, CH], U32, align_bytes=64)
         w_planes = const.tile([P, STREAMS, CH], U8, align_bytes=64)
-        bias_bf = const.tile([P, ALL_CH], BF16)
-        bias_rep = const.tile([P, MAX_SLOTS, ALL_CH], F32)
+        bias_row = const.tile([P, ALL_CH], BF16)
+        ones = const.tile([P, P], BF16)
+        bias_rep = const.tile([P, 2 * ALL_CH], F32)
         gb_rows_bf = const.tile([P, P], BF16)
         gb_rows = const.tile([P, P], F32)
         gb = const.tile([P, 2 * STREAMS], F32)
@@ -147,9 +148,9 @@ def tile_batchedgraphsagemean1_pb_t_kernel(
                         stop=True,
                     )
                 cols = slice(first * P, (first + count) * P)
+                channel = first * P % ALL_CH
                 nc.vector.tensor_tensor(
-                    out=hb[:, cols], in0=h[:, 0:count * P], in1=bias_rep[:].rearrange("p t n -> p (t n)")[:, cols],
-                    op=ALU.add,
+                    out=hb[:, cols], in0=h[:, 0:count * P], in1=bias_rep[:, channel:channel + count * P], op=ALU.add
                 )
             h_biased[i] = hb
 
@@ -203,7 +204,9 @@ def tile_batchedgraphsagemean1_pb_t_kernel(
                     nc.vector.bn_stats(out=stats[:, s, i, :], in_=of_stream(i, s))
 
         nc.vector.memset(w_planes[:].rearrange("p s n -> p (s n)").bitcast(I32), 0)
+        nc.vector.memset(bias_row[:], 0.0)
         nc.vector.memset(gb_rows_bf[:], 0.0)
+        nc.vector.memset(ones[:], 1.0)
         nc.vector.memset(tuples[:], float(FIRST_SLOT[PIECES - 1] * P))
         zero = const.tile([P, 1], F32)
         eps = const.tile([P, 1], F32)
@@ -225,14 +228,14 @@ def tile_batchedgraphsagemean1_pb_t_kernel(
                     in_=w_scales_in[s][0, 4 * quad:4 * quad + 4, :].bitcast(I32),
                 )
         for s in range(STREAMS):
-            nc.scalar.dma_start(out=bias_bf[:, s * CH:(s + 1) * CH], in_=biases_in[s].partition_broadcast(P))
-        nc.scalar.dma_start(out=gb_rows_bf[0:STREAMS, :], in_=bn_gamma.rearrange("(s o) -> s o", s=STREAMS))
-        nc.scalar.dma_start(out=gb_rows_bf[STREAMS:2 * STREAMS, :], in_=bn_beta.rearrange("(s o) -> s o", s=STREAMS))
+            nc.gpsimd.dma_start(
+                out=bias_row[0:1, s * CH:(s + 1) * CH], in_=biases_in[s].rearrange("(r o) -> r o", r=1)
+            )
+        nc.gpsimd.dma_start(out=gb_rows_bf[0:STREAMS, :], in_=bn_gamma.rearrange("(s o) -> s o", s=STREAMS))
+        nc.gpsimd.dma_start(out=gb_rows_bf[STREAMS:2 * STREAMS, :], in_=bn_beta.rearrange("(s o) -> s o", s=STREAMS))
         warm = const.tile([P, 1], F32)
         nc.vector.memset(warm[:], 1.0)
         nc.scalar.sqrt(out=warm[:], in_=warm[:])
-        for t in range(MAX_SLOTS):
-            nc.vector.tensor_copy(out=bias_rep[:, t, :], in_=bias_bf[:])
         nc.vector.tensor_copy(out=gb_rows[:], in_=gb_rows_bf[:])
 
         def run(stage, i):
@@ -252,6 +255,10 @@ def tile_batchedgraphsagemean1_pb_t_kernel(
                 gb_ps = banks.tile([P, P], F32, tag="bank", name="gb_ps")
                 nc.tensor.transpose(gb_ps[:], gb_rows[:], ident[:])
                 nc.vector.tensor_copy(out=gb[:], in_=gb_ps[:, 0:2 * STREAMS])
+                b_ps = banks.tile([P, ALL_CH], F32, tag="bank", name="b_ps")
+                nc.tensor.matmul(b_ps[:], lhsT=ones[:], rhs=bias_row[:], start=True, stop=True)
+                for k in range(2):
+                    nc.vector.tensor_copy(out=bias_rep[:, k * ALL_CH:(k + 1) * ALL_CH], in_=b_ps[:])
 
         mean_var = const.tile([P, STREAMS, 2], F32)
         for s in range(STREAMS):

@@ -260,6 +260,21 @@ def tile_batchedgraphsagemean1_pb_t_kernel(
                 for k in range(2):
                     nc.vector.tensor_copy(out=bias_rep[:, k * ALL_CH:(k + 1) * ALL_CH], in_=b_ps[:])
 
+        def keep_clock(passes):
+            unread = banks.tile([P, BANK], F32, tag="bank", name="unread")
+            for k in range(passes):
+                nc.tensor.matmul_mx(
+                    out=unread[:, 0:2 * CH],
+                    lhsT=w_codes[:, 0, :].bitcast(FP8X4),
+                    lhsT_scale=w_planes[:, 0, :],
+                    rhs=w_codes[:, 0:2, :].rearrange("p s n -> p (s n)").bitcast(FP8X4),
+                    rhs_scale=w_planes[:, 0:2, :].rearrange("p s n -> p (s n)"),
+                    start=True,
+                    stop=True,
+                )
+
+        keep_clock(12)
+
         mean_var = const.tile([P, STREAMS, 2], F32)
         for s in range(STREAMS):
             nc.vector.bn_aggr(out=mean_var[:, s, :], in_=tuples[:, s, :, :].rearrange("p a k -> p (a k)"))
@@ -314,6 +329,7 @@ def tile_batchedgraphsagemean1_pb_t_kernel(
                     nc.sync.dma_start(out=piece_out[:, cols], in_=stage[:, cols])
             if i != order[0]:
                 nc.sync.dma_start(out=piece_out, in_=stage[:, 0:n * ALL_CH])
+            keep_clock(2)
 
         scale_and_shift(order[0])
         for k in range(PIECES):

@@ -32,6 +32,9 @@ assert ALL_SLOTS * P == ROWS
 AHEAD = 2
 DEPTH = 4
 
+BIAS_TURN = 1
+GB_TURN = 5
+
 FLOPS = 2 * ROWS * FEAT * ALL_CH
 
 
@@ -89,119 +92,119 @@ def tile_batchedgraphsagemean1_pb_t_kernel(
         def rows_of(i):
             return slice(FIRST_SLOT[i] * P, (FIRST_SLOT[i] + PIECE_SLOTS[i]) * P)
 
-        def load(i):
+        def load(i, queue=nc.sync):
             n = PIECE_SLOTS[i]
             x_tiles[i] = []
             for s in range(STREAMS):
                 x_sb = xin.tile([P, MAX_SLOTS, FEAT], BF16, tag="x_sb", name="x_sb")
-                nc.sync.dma_start(out=x_sb[:, 0:n, :], in_=feats[s][rows_of(i), :].rearrange("(p t) f -> p t f", t=n))
+                queue.dma_start(out=x_sb[:, 0:n, :], in_=feats[s][rows_of(i), :].rearrange("(p t) f -> p t f", t=n))
                 x_tiles[i].append(x_sb)
 
-        def features_to_partitions(i):
+        def features_to_partitions(i, s):
             n = PIECE_SLOTS[i]
-            grouped[i] = []
-            for s in range(STREAMS):
-                x_words = x_tiles[i][s][:].bitcast(F32)
-                g = quant.tile([P, MAX_SLOTS * P * 4], BF16, align_bytes=64, tag="grouped", name="grouped")
-                g_words = g[:].bitcast(F32)
-                for first, count in bank_loads(2 * n):
-                    slots = count // 2
-                    t0 = first // 2
-                    xt = banks.tile([P, PER_BANK // 2, P, 2], F32, tag="bank", name="xt")
-                    for tt in range(slots):
-                        for u in range(2):
-                            nc.tensor.transpose(xt[:, tt, :, u], x_words[:, t0 + tt, u:WORDS:2], ident[:])
-                    dst = g_words[:, first * P:(first + count) * P]
-                    src = xt[:, 0:slots, :, :].rearrange("q tt r u -> q (tt r u)")
-                    if s == STREAMS - 1 and (first > 0 or i % 2 == 0):
-                        nc.vector.tensor_copy(out=dst, in_=src)
-                    else:
-                        nc.scalar.copy(out=dst, in_=src)
-                grouped[i].append(g)
+            x_words = x_tiles[i][s][:].bitcast(F32)
+            g = quant.tile([P, MAX_SLOTS * P * 4], BF16, align_bytes=64, tag="grouped", name="grouped")
+            g_words = g[:].bitcast(F32)
+            for first, count in bank_loads(2 * n):
+                slots = count // 2
+                t0 = first // 2
+                xt = banks.tile([P, PER_BANK // 2, P, 2], F32, tag="bank", name="xt")
+                for tt in range(slots):
+                    for u in range(2):
+                        nc.tensor.transpose(xt[:, tt, :, u], x_words[:, t0 + tt, u:WORDS:2], ident[:])
+                dst = g_words[:, first * P:(first + count) * P]
+                src = xt[:, 0:slots, :, :].rearrange("q tt r u -> q (tt r u)")
+                if s == STREAMS - 1 and (first > 0 or i % 2 == 0):
+                    nc.vector.tensor_copy(out=dst, in_=src)
+                else:
+                    nc.scalar.copy(out=dst, in_=src)
+            grouped[i, s] = g
 
-        def quantise(i):
+        def quantise(i, s):
             cols = PIECE_SLOTS[i] * P
-            codes[i] = []
-            planes[i] = []
-            for s in range(STREAMS):
-                code = quant.tile([P, MAX_SLOTS * P], U32, align_bytes=64, tag="code", name="code")
-                plane = quant.tile([P, MAX_SLOTS * P], U8, align_bytes=64, tag="plane", name="plane")
-                nc.vector.quantize_mx(
-                    out=code[:, 0:cols].bitcast(FP8X4), scales=plane[:, 0:cols], in_=grouped[i][s][:, 0:4 * cols]
-                )
-                codes[i].append(code)
-                planes[i].append(plane)
+            code = quant.tile([P, MAX_SLOTS * P], U32, align_bytes=64, tag="code", name="code")
+            plane = quant.tile([P, MAX_SLOTS * P], U8, align_bytes=64, tag="plane", name="plane")
+            nc.vector.quantize_mx(
+                out=code[:, 0:cols].bitcast(FP8X4), scales=plane[:, 0:cols], in_=grouped[i, s][:, 0:4 * cols]
+            )
+            codes[i, s] = code
+            planes[i, s] = plane
 
-        def project(i):
-            hb = rowp.tile([P, MAX_SLOTS * ALL_CH], F32, tag="hb", name="hb")
-            for first, count in bank_loads(PIECE_SLOTS[i] * STREAMS):
-                h = banks.tile([P, BANK], F32, tag="bank", name="h")
-                for k in range(count):
-                    t, s = divmod(first + k, STREAMS)
-                    nc.tensor.matmul_mx(
-                        out=h[:, k * P:(k + 1) * P],
-                        lhsT=codes[i][s][:, t * P:(t + 1) * P].bitcast(FP8X4),
-                        lhsT_scale=planes[i][s][:, t * P:(t + 1) * P],
-                        rhs=w_codes[:, s, :].bitcast(FP8X4),
-                        rhs_scale=w_planes[:, s, :],
-                        start=True,
-                        stop=True,
+        def project(i, j):
+            loads = bank_loads(PIECE_SLOTS[i] * STREAMS)
+            if j == 0:
+                h_biased[i] = rowp.tile([P, MAX_SLOTS * ALL_CH], F32, tag="hb", name="hb")
+            if j >= len(loads):
+                return
+            first, count = loads[j]
+            h = banks.tile([P, BANK], F32, tag="bank", name="h")
+            for k in range(count):
+                t, s = divmod(first + k, STREAMS)
+                nc.tensor.matmul_mx(
+                    out=h[:, k * P:(k + 1) * P],
+                    lhsT=codes[i, s][:, t * P:(t + 1) * P].bitcast(FP8X4),
+                    lhsT_scale=planes[i, s][:, t * P:(t + 1) * P],
+                    rhs=w_codes[:, s, :].bitcast(FP8X4),
+                    rhs_scale=w_planes[:, s, :],
+                    start=True,
+                    stop=True,
+                )
+            cols = slice(first * P, (first + count) * P)
+            channel = first * P % ALL_CH
+            nc.vector.tensor_tensor(
+                out=h_biased[i][:, cols], in0=h[:, 0:count * P], in1=bias_rep[:, channel:channel + count * P], op=ALU.add
+            )
+
+        def sum_squares(i, slots):
+            if i not in sumsq:
+                sumsq[i] = small.tile([P, MAX_SLOTS], F32, tag="sumsq", name="sumsq")
+            for t in slots:
+                if t < PIECE_SLOTS[i]:
+                    squares = small.tile([P, ALL_CH], F32, tag="squares", name="squares")
+                    nc.scalar.activation(
+                        out=squares[:], in_=h_biased[i][:, t * ALL_CH:(t + 1) * ALL_CH], func=ACT.Square,
+                        accum_out=sumsq[i][:, t:t + 1],
                     )
-                cols = slice(first * P, (first + count) * P)
-                channel = first * P % ALL_CH
-                nc.vector.tensor_tensor(
-                    out=hb[:, cols], in0=h[:, 0:count * P], in1=bias_rep[:, channel:channel + count * P], op=ALU.add
-                )
-            h_biased[i] = hb
-
-        def sum_squares(i):
-            sumsq[i] = small.tile([P, MAX_SLOTS], F32, tag="sumsq", name="sumsq")
-            for t in range(PIECE_SLOTS[i]):
-                squares = small.tile([P, ALL_CH], F32, tag="squares", name="squares")
-                nc.scalar.activation(
-                    out=squares[:], in_=h_biased[i][:, t * ALL_CH:(t + 1) * ALL_CH], func=ACT.Square,
-                    accum_out=sumsq[i][:, t:t + 1],
-                )
 
         def divide_by_norm(i):
             n = PIECE_SLOTS[i]
             inv_norm = small.tile([P, MAX_SLOTS], F32, tag="inv_norm", name="inv_norm")
             nc.gpsimd.tensor_scalar_max(out=inv_norm[:, 0:n], in0=sumsq[i][:, 0:n], scalar1=1e-24)
             nc.gpsimd.tensor_tensor(out=inv_norm[:, 0:n], in0=inv_norm[:, 0:n], in1=minus_half[:, 0:n], op=ALU.pow)
-            z = rowp.tile([P, MAX_SLOTS * ALL_CH], F32, tag="z", name="z")
+            z = rowp.tile([P, MAX_SLOTS, STREAMS, CH], F32, tag="z", name="z")
             for t in range(n):
                 nc.gpsimd.tensor_scalar(
-                    out=z[:, t * ALL_CH:(t + 1) * ALL_CH], in0=h_biased[i][:, t * ALL_CH:(t + 1) * ALL_CH],
+                    out=z[:, t, :, :].rearrange("p s n -> p (s n)"), in0=h_biased[i][:, t * ALL_CH:(t + 1) * ALL_CH],
                     scalar1=inv_norm[:, t:t + 1], scalar2=0.0, op0=ALU.mult, op1=ALU.add,
                 )
             scaled[i] = z
 
-        def channels_to_partitions(i):
-            for first, count in bank_loads(PIECE_SLOTS[i] * STREAMS):
-                zt = banks.tile([P, PER_BANK, P], F32, tag="bank", name="zt")
-                for k in range(count):
-                    nc.tensor.transpose(zt[:, k, :], scaled[i][:, (first + k) * P:(first + k + 1) * P], ident[:])
-                square = FIRST_SLOT[i] * STREAMS + first
-                nc.scalar.activation(out=r_ch[:, square:square + count, :], in_=zt[:, 0:count, :], func=ACT.Relu)
+        def channels_to_partitions(i, s):
+            n = PIECE_SLOTS[i]
+            zt = banks.tile([P, PER_BANK, P], F32, tag="bank", name="zt")
+            for t in range(n):
+                nc.tensor.transpose(zt[:, t, :], scaled[i][:, t, s, :], ident[:])
+            nc.scalar.activation(out=of_stream(i, s), in_=zt[:, 0:n, :], func=ACT.Relu)
 
         def of_stream(i, s):
-            squares = slice(FIRST_SLOT[i] * STREAMS, (FIRST_SLOT[i] + PIECE_SLOTS[i]) * STREAMS)
-            return r_ch[:, squares, :].rearrange("n (t s) r -> n s t r", s=STREAMS)[:, s]
+            first = FIRST_SLOT[i] * STREAMS + s * PIECE_SLOTS[i]
+            return r_ch[:, first:first + PIECE_SLOTS[i], :]
 
-        def statistics(i):
-            if i == PIECES - 1:
-                for s in range(STREAMS):
-                    nc.vector.bn_aggr(
-                        out=tuples[:, s, 0, 1:3], in_=stats[:, s, :, :].rearrange("p c k -> p (c k)")
-                    )
-                nc.vector.tensor_scalar_mul(
-                    out=tuples[:, :, 0, 2], in0=tuples[:, :, 0, 2], scalar1=float(FIRST_SLOT[i] * P)
-                )
+        def sum_up_the_others():
             for s in range(STREAMS):
-                if i == PIECES - 1:
-                    nc.vector.bn_stats(out=tuples[:, s, 1:3, :].rearrange("p a k -> p (a k)"), in_=of_stream(i, s))
-                else:
-                    nc.vector.bn_stats(out=stats[:, s, i, :], in_=of_stream(i, s))
+                nc.vector.bn_aggr(
+                    out=tuples[:, s, 0, 1:3], in_=stats[:, s, :, :].rearrange("p c k -> p (c k)")
+                )
+            nc.vector.tensor_scalar_mul(
+                out=tuples[:, :, 0, 2], in0=tuples[:, :, 0, 2], scalar1=float(FIRST_SLOT[PIECES - 1] * P)
+            )
+
+        def statistics(i, s):
+            src = of_stream(i, s).rearrange("n t r -> n (t r)")
+            if i == PIECES - 1:
+                nc.vector.bn_stats(out=tuples[:, s, 1:3, :].rearrange("p a k -> p (a k)"), in_=src)
+            else:
+                nc.vector.bn_stats(out=stats[:, s, i, :], in_=src)
 
         nc.vector.memset(w_planes[:].rearrange("p s n -> p (s n)").bitcast(I32), 0)
         nc.vector.memset(bias_row[:], 0.0)
@@ -214,13 +217,13 @@ def tile_batchedgraphsagemean1_pb_t_kernel(
         nc.vector.tensor_scalar_add(out=eps[:], in0=zero[:], scalar1=1e-5)
         make_identity(nc, ident[:])
         nc.gpsimd.memset(minus_half[:], -0.5)
-        for i in range(AHEAD):
-            load(i)
+        load(0, nc.sync)
         for s in range(STREAMS):
             nc.sync.dma_start(
                 out=w_codes[:, s, :].bitcast(I32),
                 in_=w_words_in[s][0].rearrange("p n t -> p (n t)").bitcast(I32),
             )
+        load(1, nc.sync)
         for s in range(STREAMS):
             for quad in range(4):
                 nc.sync.dma_start(
@@ -236,25 +239,34 @@ def tile_batchedgraphsagemean1_pb_t_kernel(
         warm = const.tile([P, 1], F32)
         nc.vector.memset(warm[:], 1.0)
         nc.scalar.sqrt(out=warm[:], in_=warm[:])
-        nc.vector.tensor_copy(out=gb_rows[:], in_=gb_rows_bf[:])
 
-        def run(stage, i):
+        def run(stage, i, *more):
             if 0 <= i < PIECES:
-                stage(i)
+                stage(i, *more)
 
         for turn in range(PIECES + DEPTH):
             run(load, turn + AHEAD)
-            run(project, turn - 2)
-            run(sum_squares, turn - 3)
+            for j in range(STREAMS):
+                run(quantise, turn - 1, j)
+            for j in range(STREAMS):
+                run(project, turn - 2, j)
+            run(sum_squares, turn - 3, range(MAX_SLOTS))
             run(divide_by_norm, turn - 3)
-            run(channels_to_partitions, turn - DEPTH)
-            run(quantise, turn - 1)
-            run(statistics, turn - DEPTH)
-            run(features_to_partitions, turn)
-            if turn == 0:
+            for j in range(STREAMS):
+                run(channels_to_partitions, turn - DEPTH, j)
+            if turn == PIECES - 1 + DEPTH:
+                sum_up_the_others()
+            for j in range(STREAMS):
+                run(statistics, turn - DEPTH, j)
+            for j in range(STREAMS):
+                run(features_to_partitions, turn, j)
+            if turn == 3:
+                nc.vector.tensor_copy(out=gb_rows[:], in_=gb_rows_bf[:])
+            if turn == 6:
                 gb_ps = banks.tile([P, P], F32, tag="bank", name="gb_ps")
                 nc.tensor.transpose(gb_ps[:], gb_rows[:], ident[:])
                 nc.vector.tensor_copy(out=gb[:], in_=gb_ps[:, 0:2 * STREAMS])
+            if turn == BIAS_TURN:
                 b_ps = banks.tile([P, ALL_CH], F32, tag="bank", name="b_ps")
                 nc.tensor.matmul(b_ps[:], lhsT=ones[:], rhs=bias_row[:], start=True, stop=True)
                 for k in range(2):
@@ -318,7 +330,8 @@ def tile_batchedgraphsagemean1_pb_t_kernel(
             for first, count in loads:
                 o_ps = banks.tile([P, PER_BANK, P], F32, tag="bank", name="o_ps")
                 for k in range(count):
-                    nc.tensor.transpose(o_ps[:, k, :], r_ch[:, FIRST_SLOT[i] * STREAMS + first + k, :], ident[:])
+                    slot, s = divmod(first + k, STREAMS)
+                    nc.tensor.transpose(o_ps[:, k, :], of_stream(i, s)[:, slot, :], ident[:])
                 cols = slice(first * P, (first + count) * P)
                 src = o_ps[:, 0:count, :].rearrange("p k n -> p (k n)")
                 if (first, count) == loads[-1]:

@@ -30,7 +30,7 @@ FIRST_SLOT = [sum(PIECE_SLOTS[:i]) for i in range(PIECES)]
 ALL_SLOTS = sum(PIECE_SLOTS)
 assert ALL_SLOTS * P == ROWS
 AHEAD = 2
-DEPTH = 4
+DEPTH = 5
 
 BIAS_TURN = 1
 GB_TURN = 5

@@ -24,13 +24,13 @@ PER_BANK = BANK // P
 BN_STATS = 6
 
 MAX_SLOTS = 4
-PIECE_SLOTS = [MAX_SLOTS] * 15 + [2, 1, 1]
+PIECE_SLOTS = [MAX_SLOTS] * 15 + [2, 2]
 PIECES = len(PIECE_SLOTS)
 FIRST_SLOT = [sum(PIECE_SLOTS[:i]) for i in range(PIECES)]
 ALL_SLOTS = sum(PIECE_SLOTS)
 assert ALL_SLOTS * P == ROWS
 AHEAD = 2
-DEPTH = 5
+DEPTH = 6
 
 BIAS_TURN = 1
 GB_TURN = 5
@@ -63,7 +63,7 @@ def tile_batchedgraphsagemean1_pb_t_kernel(
         const = ctx.enter_context(tc.tile_pool(name="const", bufs=1))
         xin = ctx.enter_context(tc.tile_pool(name="xin", bufs=3 * STREAMS))
         quant = ctx.enter_context(tc.tile_pool(name="quant", bufs=2 * STREAMS))
-        rowp = ctx.enter_context(tc.tile_pool(name="rowp", bufs=3))
+        rowp = ctx.enter_context(tc.tile_pool(name="rowp", bufs=4))
         small = ctx.enter_context(tc.tile_pool(name="small", bufs=4))
         banks = ctx.enter_context(tc.psum_pool(name="banks", bufs=8))
 
@@ -248,16 +248,16 @@ def tile_batchedgraphsagemean1_pb_t_kernel(
             run(load, turn + AHEAD)
             for j in range(STREAMS):
                 run(quantise, turn - 1, j)
-            for j in range(STREAMS):
-                run(project, turn - 2, j)
             run(sum_squares, turn - 3, range(MAX_SLOTS))
             run(divide_by_norm, turn - 3)
             for j in range(STREAMS):
-                run(channels_to_partitions, turn - DEPTH, j)
-            if turn == PIECES - 1 + DEPTH:
+                run(channels_to_partitions, turn - 6, j)
+            for j in range(STREAMS):
+                run(project, turn - 2, j)
+            if turn == PIECES - 1 + 6:
                 sum_up_the_others()
             for j in range(STREAMS):
-                run(statistics, turn - DEPTH, j)
+                run(statistics, turn - 6, j)
             for j in range(STREAMS):
                 run(features_to_partitions, turn, j)
             if turn == 3:

@@ -103,32 +103,39 @@ def tile_batchedgraphsagemean1_pb_t_kernel(
         def features_to_partitions(i, s):
             n = PIECE_SLOTS[i]
             x_words = x_tiles[i][s][:].bitcast(F32)
-            g = quant.tile([P, MAX_SLOTS * P * 4], BF16, align_bytes=64, tag="grouped", name="grouped")
-            g_words = g[:].bitcast(F32)
+            if s == 0:
+                grouped[i, 0] = quant.tile([P, 2 * MAX_SLOTS * P * 4], BF16, align_bytes=64, tag="grouped2", name="grouped2", bufs=2)
+            if s == 2:
+                grouped[i, 2] = quant.tile([P, MAX_SLOTS * P * 4], BF16, align_bytes=64, tag="grouped", name="grouped", bufs=2)
+            at = n * P * 2 if s == 1 else 0
+            g_words = grouped[i, 0 if s < 2 else 2][:].bitcast(F32)[:, at:at + n * P * 2]
             for first, count in bank_loads(2 * n):
                 slots = count // 2
                 t0 = first // 2
-                xt = banks.tile([P, PER_BANK // 2, P, 2], F32, tag="bank", name="xt")
+                xt = banks.tile([P, PER_BANK // 2, 2, P], F32, tag="bank", name="xt")
                 for tt in range(slots):
                     for u in range(2):
-                        nc.tensor.transpose(xt[:, tt, :, u], x_words[:, t0 + tt, u:WORDS:2], ident[:])
-                dst = g_words[:, first * P:(first + count) * P]
-                src = xt[:, 0:slots, :, :].rearrange("q tt r u -> q (tt r u)")
+                        nc.tensor.transpose(xt[:, tt, u, :], x_words[:, t0 + tt, u:WORDS:2], ident[:])
+                dst = g_words[:, first * P:(first + count) * P].rearrange("q (tt r u) -> q tt r u", tt=slots, u=2)
+                src = xt[:, 0:slots, :, :].rearrange("q tt u r -> q tt r u")
                 if s == STREAMS - 1 and (first > 0 or i % 2 == 0):
                     nc.vector.tensor_copy(out=dst, in_=src)
                 else:
                     nc.scalar.copy(out=dst, in_=src)
-            grouped[i, s] = g
 
         def quantise(i, s):
-            cols = PIECE_SLOTS[i] * P
-            code = quant.tile([P, MAX_SLOTS * P], U32, align_bytes=64, tag="code", name="code")
-            plane = quant.tile([P, MAX_SLOTS * P], U8, align_bytes=64, tag="plane", name="plane")
+            if s == 1:
+                return
+            cols = PIECE_SLOTS[i] * P * (2 if s == 0 else 1)
+            code = quant.tile([P, (2 if s == 0 else 1) * MAX_SLOTS * P], U32, align_bytes=64, tag="code%d" % s, name="code", bufs=2)
+            plane = quant.tile([P, (2 if s == 0 else 1) * MAX_SLOTS * P], U8, align_bytes=64, tag="plane%d" % s, name="plane", bufs=2)
             nc.vector.quantize_mx(
                 out=code[:, 0:cols].bitcast(FP8X4), scales=plane[:, 0:cols], in_=grouped[i, s][:, 0:4 * cols]
             )
-            codes[i, s] = code
-            planes[i, s] = plane
+            for k in range(2 if s == 0 else 1):
+                part = slice(k * PIECE_SLOTS[i] * P, (k + 1) * PIECE_SLOTS[i] * P)
+                codes[i, s + k] = code[:, part]
+                planes[i, s + k] = plane[:, part]
 
         def project(i, j):
             loads = bank_loads(PIECE_SLOTS[i] * STREAMS)
@@ -310,17 +317,20 @@ def tile_batchedgraphsagemean1_pb_t_kernel(
         order = list(range(PIECES))
 
         def scale_and_shift(i):
-            for s in range(STREAMS):
-                if i == order[0] and s == STREAMS - 1:
-                    nc.scalar.activation(
-                        out=of_stream(i, s), in_=of_stream(i, s), func=ACT.Identity,
-                        scale=scale[:, s:s + 1], bias=shift[:, s:s + 1],
-                    )
-                else:
-                    nc.vector.tensor_scalar(
-                        out=of_stream(i, s), in0=of_stream(i, s), scalar1=scale[:, s:s + 1], scalar2=shift[:, s:s + 1],
-                        op0=ALU.mult, op1=ALU.add,
-                    )
+            n = PIECE_SLOTS[i]
+            parts = [slice(t, t + 1) for t in range(n)] if i == order[0] else [slice(0, n)]
+            for part in parts:
+                for s in range(STREAMS):
+                    r = of_stream(i, s)[:, part, :]
+                    if i == order[0] and s == STREAMS - 1:
+                        nc.scalar.activation(
+                            out=r, in_=r, func=ACT.Identity, scale=scale[:, s:s + 1], bias=shift[:, s:s + 1]
+                        )
+                    else:
+                        nc.vector.tensor_scalar(
+                            out=r, in0=r, scalar1=scale[:, s:s + 1], scalar2=shift[:, s:s + 1],
+                            op0=ALU.mult, op1=ALU.add,
+                        )
 
         def rows_to_partitions_and_store(i):
             n = PIECE_SLOTS[i]

from contextlib import ExitStack

import concourse.mybir as mybir
from concourse.masks import make_identity

F32 = mybir.dt.float32
BF16 = mybir.dt.bfloat16
I32 = mybir.dt.int32
U32 = mybir.dt.uint32
U8 = mybir.dt.uint8
FP8X4 = mybir.dt.float8_e4m3fn_x4
ALU = mybir.AluOpType
ACT = mybir.ActivationFunctionType

P = 128
ROWS = 8 * 512 * 2
FEAT = 512
CH = 128
STREAMS = 3
ALL_CH = STREAMS * CH
WORDS = FEAT // 2
BANK = 512
PER_BANK = BANK // P
BN_STATS = 6

MAX_SLOTS = 4
PIECE_SLOTS = [MAX_SLOTS] * 15 + [2, 2]
PIECES = len(PIECE_SLOTS)
FIRST_SLOT = [sum(PIECE_SLOTS[:i]) for i in range(PIECES)]
ALL_SLOTS = sum(PIECE_SLOTS)
assert ALL_SLOTS * P == ROWS
AHEAD = 2
DEPTH = 6

BIAS_TURN = 1
GB_TURN = 5

FLOPS = 2 * ROWS * FEAT * ALL_CH


def bank_loads(squares):
    return [(first, min(PER_BANK, squares - first)) for first in range(0, squares, PER_BANK)]


def tile_batchedgraphsagemean1_pb_t_kernel(
    tc,
    x, nb, mu,
    wx_words, wx_scales, wx_b,
    wn_words, wn_scales, wn_b,
    wr_words, wr_scales, wr_b,
    bn_gamma, bn_beta,
    out,
):
    nc = tc.nc
    feats = [x.flatten_outer_dims(), nb.flatten_outer_dims(), mu.flatten_outer_dims()]
    w_words_in = [wx_words, wn_words, wr_words]
    w_scales_in = [wx_scales, wn_scales, wr_scales]
    biases_in = [wx_b, wn_b, wr_b]
    out_rows = out.flatten_outer_dims()

    with ExitStack() as ctx:
        ctx.enter_context(tc.manual_schedule())
        const = ctx.enter_context(tc.tile_pool(name="const", bufs=1))
        xin = ctx.enter_context(tc.tile_pool(name="xin", bufs=3 * STREAMS))
        quant = ctx.enter_context(tc.tile_pool(name="quant", bufs=2 * STREAMS))
        rowp = ctx.enter_context(tc.tile_pool(name="rowp", bufs=4))
        small = ctx.enter_context(tc.tile_pool(name="small", bufs=4))
        banks = ctx.enter_context(tc.psum_pool(name="banks", bufs=8))

        ident = const.tile([P, P], F32)
        w_codes = const.tile([P, STREAMS, CH], U32, align_bytes=64)
        w_planes = const.tile([P, STREAMS, CH], U8, align_bytes=64)
        bias_row = const.tile([P, ALL_CH], BF16)
        ones = const.tile([P, P], BF16)
        bias_rep = const.tile([P, 2 * ALL_CH], F32)
        gb_rows_bf = const.tile([P, P], BF16)
        gb_rows = const.tile([P, P], F32)
        gb = const.tile([P, 2 * STREAMS], F32)
        minus_half = const.tile([P, MAX_SLOTS], F32)
        r_ch = const.tile([P, ALL_SLOTS * STREAMS, P], F32)
        stats = const.tile([P, STREAMS, PIECES - 1, BN_STATS], F32)
        tuples = const.tile([P, STREAMS, 3, BN_STATS // 2], F32)

        x_tiles = {}
        grouped = {}
        codes = {}
        planes = {}
        h_biased = {}
        sumsq = {}
        scaled = {}

        def rows_of(i):
            return slice(FIRST_SLOT[i] * P, (FIRST_SLOT[i] + PIECE_SLOTS[i]) * P)

        def load(i, queue=nc.sync):
            n = PIECE_SLOTS[i]
            x_tiles[i] = []
            for s in range(STREAMS):
                x_sb = xin.tile([P, MAX_SLOTS, FEAT], BF16, tag="x_sb", name="x_sb")
                queue.dma_start(out=x_sb[:, 0:n, :], in_=feats[s][rows_of(i), :].rearrange("(p t) f -> p t f", t=n))
                x_tiles[i].append(x_sb)

        def features_to_partitions(i, s):
            n = PIECE_SLOTS[i]
            x_words = x_tiles[i][s][:].bitcast(F32)
            if s == 0:
                grouped[i, 0] = quant.tile([P, 2 * MAX_SLOTS * P * 4], BF16, align_bytes=64, tag="grouped2", name="grouped2", bufs=2)
            if s == 2:
                grouped[i, 2] = quant.tile([P, MAX_SLOTS * P * 4], BF16, align_bytes=64, tag="grouped", name="grouped", bufs=2)
            at = n * P * 2 if s == 1 else 0
            g_words = grouped[i, 0 if s < 2 else 2][:].bitcast(F32)[:, at:at + n * P * 2]
            for first, count in bank_loads(2 * n):
                slots = count // 2
                t0 = first // 2
                xt = banks.tile([P, PER_BANK // 2, 2, P], F32, tag="bank", name="xt")
                for tt in range(slots):
                    for u in range(2):
                        nc.tensor.transpose(xt[:, tt, u, :], x_words[:, t0 + tt, u:WORDS:2], ident[:])
                dst = g_words[:, first * P:(first + count) * P].rearrange("q (tt r u) -> q tt r u", tt=slots, u=2)
                src = xt[:, 0:slots, :, :].rearrange("q tt u r -> q tt r u")
                if s == STREAMS - 1 and (first > 0 or i % 2 == 0):
                    nc.vector.tensor_copy(out=dst, in_=src)
                else:
                    nc.scalar.copy(out=dst, in_=src)

        def quantise(i, s):
            if s == 1:
                return
            cols = PIECE_SLOTS[i] * P * (2 if s == 0 else 1)
            code = quant.tile([P, (2 if s == 0 else 1) * MAX_SLOTS * P], U32, align_bytes=64, tag="code%d" % s, name="code", bufs=2)
            plane = quant.tile([P, (2 if s == 0 else 1) * MAX_SLOTS * P], U8, align_bytes=64, tag="plane%d" % s, name="plane", bufs=2)
            nc.vector.quantize_mx(
                out=code[:, 0:cols].bitcast(FP8X4), scales=plane[:, 0:cols], in_=grouped[i, s][:, 0:4 * cols]
            )
            for k in range(2 if s == 0 else 1):
                part = slice(k * PIECE_SLOTS[i] * P, (k + 1) * PIECE_SLOTS[i] * P)
                codes[i, s + k] = code[:, part]
                planes[i, s + k] = plane[:, part]

        def project(i, j):
            loads = bank_loads(PIECE_SLOTS[i] * STREAMS)
            if j == 0:
                h_biased[i] = rowp.tile([P, MAX_SLOTS * ALL_CH], F32, tag="hb", name="hb")
            if j >= len(loads):
                return
            first, count = loads[j]
            h = banks.tile([P, BANK], F32, tag="bank", name="h")
            for k in range(count):
                t, s = divmod(first + k, STREAMS)
                nc.tensor.matmul_mx(
                    out=h[:, k * P:(k + 1) * P],
                    lhsT=codes[i, s][:, t * P:(t + 1) * P].bitcast(FP8X4),
                    lhsT_scale=planes[i, s][:, t * P:(t + 1) * P],
                    rhs=w_codes[:, s, :].bitcast(FP8X4),
                    rhs_scale=w_planes[:, s, :],
                    start=True,
                    stop=True,
                )
            cols = slice(first * P, (first + count) * P)
            channel = first * P % ALL_CH
            nc.vector.tensor_tensor(
                out=h_biased[i][:, cols], in0=h[:, 0:count * P], in1=bias_rep[:, channel:channel + count * P], op=ALU.add
            )

        def sum_squares(i, slots):
            if i not in sumsq:
                sumsq[i] = small.tile([P, MAX_SLOTS], F32, tag="sumsq", name="sumsq")
            for t in slots:
                if t < PIECE_SLOTS[i]:
                    squares = small.tile([P, ALL_CH], F32, tag="squares", name="squares")
                    nc.scalar.activation(
                        out=squares[:], in_=h_biased[i][:, t * ALL_CH:(t + 1) * ALL_CH], func=ACT.Square,
                        accum_out=sumsq[i][:, t:t + 1],
                    )

        def divide_by_norm(i):
            n = PIECE_SLOTS[i]
            inv_norm = small.tile([P, MAX_SLOTS], F32, tag="inv_norm", name="inv_norm")
            nc.gpsimd.tensor_scalar_max(out=inv_norm[:, 0:n], in0=sumsq[i][:, 0:n], scalar1=1e-24)
            nc.gpsimd.tensor_tensor(out=inv_norm[:, 0:n], in0=inv_norm[:, 0:n], in1=minus_half[:, 0:n], op=ALU.pow)
            z = rowp.tile([P, MAX_SLOTS, STREAMS, CH], F32, tag="z", name="z")
            for t in range(n):
                nc.gpsimd.tensor_scalar(
                    out=z[:, t, :, :].rearrange("p s n -> p (s n)"), in0=h_biased[i][:, t * ALL_CH:(t + 1) * ALL_CH],
                    scalar1=inv_norm[:, t:t + 1], scalar2=0.0, op0=ALU.mult, op1=ALU.add,
                )
            scaled[i] = z

        def channels_to_partitions(i, s):
            n = PIECE_SLOTS[i]
            zt = banks.tile([P, PER_BANK, P], F32, tag="bank", name="zt")
            for t in range(n):
                nc.tensor.transpose(zt[:, t, :], scaled[i][:, t, s, :], ident[:])
            nc.scalar.activation(out=of_stream(i, s), in_=zt[:, 0:n, :], func=ACT.Relu)

        def of_stream(i, s):
            first = FIRST_SLOT[i] * STREAMS + s * PIECE_SLOTS[i]
            return r_ch[:, first:first + PIECE_SLOTS[i], :]

        def sum_up_the_others():
            for s in range(STREAMS):
                nc.vector.bn_aggr(
                    out=tuples[:, s, 0, 1:3], in_=stats[:, s, :, :].rearrange("p c k -> p (c k)")
                )
            nc.vector.tensor_scalar_mul(
                out=tuples[:, :, 0, 2], in0=tuples[:, :, 0, 2], scalar1=float(FIRST_SLOT[PIECES - 1] * P)
            )

        def statistics(i, s):
            src = of_stream(i, s).rearrange("n t r -> n (t r)")
            if i == PIECES - 1:
                nc.vector.bn_stats(out=tuples[:, s, 1:3, :].rearrange("p a k -> p (a k)"), in_=src)
            else:
                nc.vector.bn_stats(out=stats[:, s, i, :], in_=src)

        nc.vector.memset(w_planes[:].rearrange("p s n -> p (s n)").bitcast(I32), 0)
        nc.vector.memset(bias_row[:], 0.0)
        nc.vector.memset(gb_rows_bf[:], 0.0)
        nc.vector.memset(ones[:], 1.0)
        nc.vector.memset(tuples[:], float(FIRST_SLOT[PIECES - 1] * P))
        zero = const.tile([P, 1], F32)
        eps = const.tile([P, 1], F32)
        nc.vector.memset(zero[:], 0.0)
        nc.vector.tensor_scalar_add(out=eps[:], in0=zero[:], scalar1=1e-5)
        make_identity(nc, ident[:])
        nc.gpsimd.memset(minus_half[:], -0.5)
        load(0, nc.sync)
        for s in range(STREAMS):
            nc.sync.dma_start(
                out=w_codes[:, s, :].bitcast(I32),
                in_=w_words_in[s][0].rearrange("p n t -> p (n t)").bitcast(I32),
            )
        load(1, nc.sync)
        for s in range(STREAMS):
            for quad in range(4):
                nc.sync.dma_start(
                    out=w_planes[32 * quad:32 * quad + 4, s, :].bitcast(I32),
                    in_=w_scales_in[s][0, 4 * quad:4 * quad + 4, :].bitcast(I32),
                )
        for s in range(STREAMS):
            nc.gpsimd.dma_start(
                out=bias_row[0:1, s * CH:(s + 1) * CH], in_=biases_in[s].rearrange("(r o) -> r o", r=1)
            )
        nc.gpsimd.dma_start(out=gb_rows_bf[0:STREAMS, :], in_=bn_gamma.rearrange("(s o) -> s o", s=STREAMS))
        nc.gpsimd.dma_start(out=gb_rows_bf[STREAMS:2 * STREAMS, :], in_=bn_beta.rearrange("(s o) -> s o", s=STREAMS))
        warm = const.tile([P, 1], F32)
        nc.vector.memset(warm[:], 1.0)
        nc.scalar.sqrt(out=warm[:], in_=warm[:])

        def run(stage, i, *more):
            if 0 <= i < PIECES:
                stage(i, *more)

        for turn in range(PIECES + DEPTH):
            run(load, turn + AHEAD)
            for j in range(STREAMS):
                run(quantise, turn - 1, j)
            run(sum_squares, turn - 3, range(MAX_SLOTS))
            run(divide_by_norm, turn - 3)
            for j in range(STREAMS):
                run(channels_to_partitions, turn - 6, j)
            for j in range(STREAMS):
                run(project, turn - 2, j)
            if turn == PIECES - 1 + 6:
                sum_up_the_others()
            for j in range(STREAMS):
                run(statistics, turn - 6, j)
            for j in range(STREAMS):
                run(features_to_partitions, turn, j)
            if turn == 3:
                nc.vector.tensor_copy(out=gb_rows[:], in_=gb_rows_bf[:])
            if turn == 6:
                gb_ps = banks.tile([P, P], F32, tag="bank", name="gb_ps")
                nc.tensor.transpose(gb_ps[:], gb_rows[:], ident[:])
                nc.vector.tensor_copy(out=gb[:], in_=gb_ps[:, 0:2 * STREAMS])
            if turn == BIAS_TURN:
                b_ps = banks.tile([P, ALL_CH], F32, tag="bank", name="b_ps")
                nc.tensor.matmul(b_ps[:], lhsT=ones[:], rhs=bias_row[:], start=True, stop=True)
                for k in range(2):
                    nc.vector.tensor_copy(out=bias_rep[:, k * ALL_CH:(k + 1) * ALL_CH], in_=b_ps[:])

        def keep_clock(passes):
            unread = banks.tile([P, BANK], F32, tag="bank", name="unread")
            for k in range(passes):
                nc.tensor.matmul_mx(
                    out=unread[:, 0:2 * CH],
                    lhsT=w_codes[:, 0, :].bitcast(FP8X4),
                    lhsT_scale=w_planes[:, 0, :],
                    rhs=w_codes[:, 0:2, :].rearrange("p s n -> p (s n)").bitcast(FP8X4),
                    rhs_scale=w_planes[:, 0:2, :].rearrange("p s n -> p (s n)"),
                    start=True,
                    stop=True,
                )

        keep_clock(12)

        mean_var = const.tile([P, STREAMS, 2], F32)
        for s in range(STREAMS):
            nc.vector.bn_aggr(out=mean_var[:, s, :], in_=tuples[:, s, :, :].rearrange("p a k -> p (a k)"))
        std = const.tile([P, STREAMS], F32)
        inv_std = const.tile([P, STREAMS], F32)
        minus_mean_gamma = const.tile([P, STREAMS], F32)
        scale = const.tile([P, STREAMS], F32)
        shift = const.tile([P, STREAMS], F32)
        nc.scalar.activation(out=std[:], in_=mean_var[:, :, 1], func=ACT.Sqrt, bias=eps[:, 0:1])
        nc.vector.scalar_tensor_tensor(
            out=minus_mean_gamma[:], in0=mean_var[:, :, 0], scalar=-1.0, in1=gb[:, 0:STREAMS], op0=ALU.mult, op1=ALU.mult
        )
        nc.vector.reciprocal(out=inv_std[:], in_=std[:])
        nc.vector.tensor_tensor(out=scale[:], in0=inv_std[:], in1=gb[:, 0:STREAMS], op=ALU.mult)
        for s in range(STREAMS):
            nc.vector.scalar_tensor_tensor(
                out=shift[:, s:s + 1], in0=minus_mean_gamma[:, s:s + 1], scalar=inv_std[:, s:s + 1],
                in1=gb[:, STREAMS + s:STREAMS + s + 1], op0=ALU.mult, op1=ALU.add,
            )

        order = list(range(PIECES))

        def scale_and_shift(i):
            n = PIECE_SLOTS[i]
            parts = [slice(t, t + 1) for t in range(n)] if i == order[0] else [slice(0, n)]
            for part in parts:
                for s in range(STREAMS):
                    r = of_stream(i, s)[:, part, :]
                    if i == order[0] and s == STREAMS - 1:
                        nc.scalar.activation(
                            out=r, in_=r, func=ACT.Identity, scale=scale[:, s:s + 1], bias=shift[:, s:s + 1]
                        )
                    else:
                        nc.vector.tensor_scalar(
                            out=r, in0=r, scalar1=scale[:, s:s + 1], scalar2=shift[:, s:s + 1],
                            op0=ALU.mult, op1=ALU.add,
                        )

        def rows_to_partitions_and_store(i):
            n = PIECE_SLOTS[i]
            loads = bank_loads(n * STREAMS)
            piece_out = out_rows[rows_of(i), :].rearrange("(p t) n -> p (t n)", t=n)
            stage = rowp.tile([P, MAX_SLOTS * ALL_CH], F32, tag="z" if i % 2 == 0 else "hb", name="stage")
            for first, count in loads:
                o_ps = banks.tile([P, PER_BANK, P], F32, tag="bank", name="o_ps")
                for k in range(count):
                    slot, s = divmod(first + k, STREAMS)
                    nc.tensor.transpose(o_ps[:, k, :], of_stream(i, s)[:, slot, :], ident[:])
                cols = slice(first * P, (first + count) * P)
                src = o_ps[:, 0:count, :].rearrange("p k n -> p (k n)")
                if (first, count) == loads[-1]:
                    nc.vector.tensor_copy(out=stage[:, cols], in_=src)
                else:
                    nc.scalar.copy(out=stage[:, cols], in_=src)
                if i == order[0]:
                    nc.sync.dma_start(out=piece_out[:, cols], in_=stage[:, cols])
            if i != order[0]:
                nc.sync.dma_start(out=piece_out, in_=stage[:, 0:n * ALL_CH])
            keep_clock(2)

        scale_and_shift(order[0])
        for k in range(PIECES):
            if k + 1 < PIECES:
                scale_and_shift(order[k + 1])
            rows_to_partitions_and_store(order[k])
